import numpy as np
import ml_dtypes


def mxq(x, axis, fmt="e4m3"):
    dtype, down = {"e4m3": (ml_dtypes.float8_e4m3fn, 7), "e5m2": (ml_dtypes.float8_e5m2, 14)}[fmt]
    v = np.moveaxis(np.asarray(x, np.float32).astype(ml_dtypes.bfloat16).astype(np.float64), axis, -1)
    blocks = v.reshape(v.shape[:-1] + (-1, 32))
    amax = np.abs(blocks).max(-1, keepdims=True)
    byte = np.maximum(np.where(amax > 0, np.frexp(amax)[1] - 1 + 127, 0) - down, 1)
    scale = np.exp2(byte - 127.0)
    codes = (blocks / scale).astype(np.float32).astype(dtype).astype(np.float64)
    return np.moveaxis((codes * scale).reshape(v.shape), -1, axis)


WIDE = False


def mx_kscale(k):
    if not WIDE:
        return np.ones(k)
    levels = np.array([10, -10, 5, -5, 0])
    a = np.random.permutation(np.resize(levels, k // 512 * 4)).reshape(k // 512, 4)
    idx = np.arange(k)
    return np.exp2(a[idx // 512, idx % 128 // 32])


BF16 = ml_dtypes.bfloat16


def bf(x):
    return np.asarray(x, np.float32).astype(BF16)


def f64(x):
    return np.asarray(x).astype(np.float64)


B, S, H, NH, NS, D = 4, 256, 2048, 16, 512, 128
TAU_LOW = 0.5
TAU_HIGH = 2.0
GATE_CAP = 0.8


def draw_primary_weights():
    u = np.random.uniform(size=(B, NH, S, S))
    diffuse = u / u.sum(-1, keepdims=True)
    sharp = np.random.uniform(size=(B, 1, S, 1))
    lam = 0.5 * sharp**2 * (0.5 + np.random.uniform(size=(B, NH, S, 1)))
    peak = np.random.randint(0, S, size=(B, 1, S, 1))
    spike = np.arange(S) == peak
    return bf((1.0 - lam) * spike + lam * diffuse)


def setup_inputs():
    t = mx_kscale(NS)
    return {"query": bf(np.random.standard_normal((B, S, D))),
            "aux_keys": bf(np.random.standard_normal((NS, D)) * 1.5),
            "aux_values": bf(np.random.standard_normal((NS, H)) * 0.25 * np.sqrt(NS) * (t.mean() / t)[:, None]),
            "reliability": bf(np.random.uniform(0.05, 1.0, NS) * t),
            "primary_attention_weights": draw_primary_weights(),
            "primary_attention_output": bf(np.random.standard_normal((B, S, H))),
            "gate_w1": bf(2.5 + 0.1 * np.random.standard_normal(1)),
            "gate_bias": bf(-1.0 + 0.1 * np.random.standard_normal(1))}


def reference(query, aux_keys, aux_values, reliability, primary_attention_weights, primary_attention_output, gate_w1, gate_bias):
    scores = f64(query) @ f64(aux_keys).T / np.sqrt(D)
    scores = scores + np.log(f64(reliability) + 1e-10)
    e = np.exp(scores - scores.max(-1, keepdims=True))
    attn_weights = e / e.sum(-1, keepdims=True)
    aux_output = mxq(attn_weights, 2, "e4m3") @ mxq(f64(aux_values), 0, "e4m3")
    avg_w = f64(primary_attention_weights).mean(axis=1)
    entropy = -(avg_w * np.log(avg_w + 1e-10)).sum(-1)
    gate = 1.0 / (1.0 + np.exp(-(f64(gate_w1) * entropy + f64(gate_bias))))
    gate = np.where(entropy < TAU_LOW, np.zeros_like(gate), gate)
    gate = np.where(entropy > TAU_HIGH, np.minimum(gate, GATE_CAP), gate)
    return f64(primary_attention_output) + gate[..., None] * aux_output

@@ -1,0 +1,370 @@
+import math
+from contextlib import ExitStack
+
+import concourse.mybir as mybir
+from concourse.masks import make_identity
+
+F32 = mybir.dt.float32
+BF16 = mybir.dt.bfloat16
+U32 = mybir.dt.uint32
+U8 = mybir.dt.uint8
+FP8X4 = mybir.dt.float8_e4m3fn_x4
+ALU = mybir.AluOpType
+FUNC = mybir.ActivationFunctionType
+AXIS_X = mybir.AxisListType.X
+
+P = 128
+PACK = 4
+B, S, H, NH, NS, D = 4, 256, 2048, 16, 512, 128
+TT = S // P
+N_TILE = 512
+N_TILES = H // N_TILE
+KH = S // P
+S_HI = P // NH
+S_LO = S // S_HI
+TAU_LOW = 0.5
+TAU_HIGH = 2.0
+GATE_CAP = 0.8
+EPS = 1e-10
+AHEAD = 2
+LOG2_E = 1.0 / math.log(2.0)
+
+FLOPS = 2 * B * S * NS * (D + H)
+
+
+def tile_auxiliarygovernedattention_pa_kernel(
+    tc,
+    query,
+    aux_keys,
+    aux_values,
+    reliability,
+    primary_attention_weights,
+    primary_attention_output,
+    gate_w1,
+    gate_bias,
+    out,
+):
+    nc = tc.nc
+    with ExitStack() as ctx:
+        ctx.enter_context(tc.manual_schedule())
+        const = ctx.enter_context(tc.tile_pool(name="const", bufs=1))
+        resident = ctx.enter_context(tc.tile_pool(name="resident", bufs=1))
+        work = ctx.enter_context(tc.tile_pool(name="work", bufs=2))
+        psum = ctx.enter_context(tc.psum_pool(name="psum", bufs=1))
+
+        def bank(shape, dtype, name):
+            return psum.tile(shape, dtype, name=name, tag="bank", bufs=6)
+
+        rel_rows = const.tile([P, NS], BF16)
+        nc.vector.memset(rel_rows[:], 0.0)
+        keys_sb = resident.tile([P, PACK, D], BF16)
+        nc.sync.dma_start(out=keys_sb[:], in_=aux_keys.rearrange("(p c) d -> p c d", c=PACK))
+        q_sb = resident.tile([P, B, TT, D], BF16)
+        nc.sync.dma_start(out=q_sb[:], in_=query.rearrange("b (p t) d -> p b t d", t=TT))
+        nc.sync.dma_start(out=rel_rows[0:1, :], in_=reliability.rearrange("(o n) -> o n", o=1))
+        w1_bf = const.tile([P, 1], BF16)
+        bias_bf = const.tile([P, 1], BF16)
+        nc.sync.dma_start(out=w1_bf[:], in_=gate_w1.partition_broadcast(P))
+        nc.sync.dma_start(out=bias_bf[:], in_=gate_bias.partition_broadcast(P))
+        val_raw = resident.tile([P, PACK, H], BF16)
+        nc.sync.dma_start(out=val_raw[:], in_=aux_values.rearrange("(p j) w -> p j w", j=PACK))
+        paw_view = primary_attention_weights.rearrange("b h (sh sl) k -> b (h sh) sl k", sh=S_HI)
+        pao_view = primary_attention_output.rearrange("b (p t) h -> b p t h", t=TT)
+        out_view = out.rearrange("b (p t) h -> b p t h", t=TT)
+        paw_sb = []
+        pao_sb = []
+        for b in range(B):
+            paw_sb.append(resident.tile([P, S_LO, S], BF16, name="paw%d" % b, tag="stream", bufs=B))
+            nc.sync.dma_start(out=paw_sb[b][:], in_=paw_view[b])
+            pao_sb.append(resident.tile([P, TT, H], BF16, name="pao%d" % b))
+            nc.sync.dma_start(out=pao_sb[b][:], in_=pao_view[b])
+
+        ident = const.tile([P, P], BF16)
+        make_identity(nc, ident[:])
+        ones = const.tile([P, P], BF16)
+        nc.vector.memset(ones[:], 1.0)
+        eps = const.tile([P, 1], F32)
+        nc.vector.memset(eps[:], EPS)
+        minus_ones = const.tile([P, 1], F32)
+        nc.vector.memset(minus_ones[:], -1.0)
+        head_count = const.tile([P, S_HI], F32)
+        nc.vector.tensor_reduce(
+            out=head_count[:],
+            in_=ident[:].rearrange("p (h n) -> p n h", n=S_HI),
+            axis=AXIS_X,
+            op=ALU.add,
+        )
+        head_mean_sel = const.tile([P, S_HI], BF16)
+        nc.vector.tensor_scalar_mul(out=head_mean_sel[:], in0=head_count[:], scalar1=1.0 / NH)
+        w1_neg = const.tile([P, 1], F32)
+        nc.gpsimd.tensor_scalar(
+            out=w1_neg[:], in0=w1_bf[:], scalar1=-LOG2_E, scalar2=0.0, op0=ALU.mult, op1=ALU.add
+        )
+        bias_neg = const.tile([P, 1], F32)
+        nc.gpsimd.tensor_scalar(
+            out=bias_neg[:], in0=bias_bf[:], scalar1=-LOG2_E, scalar2=0.0, op0=ALU.mult, op1=ALU.add
+        )
+        twos = const.tile([P, TT], F32)
+        nc.gpsimd.memset(twos[:], 2.0)
+
+        keys_ps = bank([P, PACK, P], BF16, "keys_ps")
+        for c in range(PACK):
+            nc.tensor.transpose(keys_ps[:, c, :], keys_sb[:, c, :], ident[:])
+        keys_t = resident.tile([P, PACK, P], BF16)
+        nc.vector.tensor_copy(out=keys_t[:], in_=keys_ps[:])
+        q_ps = bank([P, B * TT, P], BF16, "q_ps")
+        for b in range(B):
+            for t in range(TT):
+                nc.tensor.transpose(q_ps[:, b * TT + t, :], q_sb[:, b, t, :], ident[:])
+        q_t = resident.tile([P, B * TT, P], BF16)
+        nc.vector.tensor_copy(out=q_t[:], in_=q_ps[:])
+
+        rel_ps = bank([P, NS], F32, "rel_ps")
+        nc.tensor.matmul(rel_ps[:], lhsT=ones[:], rhs=rel_rows[:], start=True, stop=True)
+        log_rel = resident.tile([P, PACK, P], F32)
+        nc.scalar.activation(
+            out=log_rel[:],
+            in_=rel_ps[:].rearrange("p (j c) -> p c j", c=PACK),
+            func=FUNC.Ln,
+            bias=eps[:],
+            scale=1.0,
+        )
+
+        attn_codes = resident.tile([P, B * TT * P], U32, align_bytes=64)
+        attn_scales = resident.tile([P, B * TT * P], U8, align_bytes=64)
+        val_codes = resident.tile([P, H], U32, align_bytes=64)
+        val_scales = resident.tile([P, H], U8, align_bytes=64)
+
+        score_ps = {}
+        expd = {}
+        exp_sum = {}
+        attn_ps = {}
+        attn_grouped = {}
+        val_grouped = {}
+        avg_ps = {}
+        log_avg = {}
+        ent_ps = {}
+        limit = {}
+        two_to_x = {}
+        gate = {}
+        aux_ps = {}
+        mixed = {}
+
+        def scores(b):
+            for t in range(TT):
+                score_ps[(b, t)] = bank([P, NS], F32, "score_ps")
+                nc.tensor.matmul(
+                    score_ps[(b, t)][:],
+                    lhsT=q_t[:, b * TT + t, :],
+                    rhs=keys_t[:].rearrange("d c j -> d (c j)"),
+                    start=True,
+                    stop=True,
+                )
+
+        def exponentials(b):
+            logits = work.tile([P, TT, NS], F32)
+            neg_max = work.tile([P, TT], F32)
+            expd[b] = work.tile([P, TT, NS], F32, name="expd")
+            exp_sum[b] = work.tile([P, TT], F32, name="exp_sum")
+            for t in range(TT):
+                nc.vector.scalar_tensor_tensor(
+                    out=logits[:, t, :],
+                    in0=score_ps[(b, t)][:],
+                    scalar=1.0 / math.sqrt(D),
+                    in1=log_rel[:].rearrange("p c j -> p (c j)"),
+                    op0=ALU.mult,
+                    op1=ALU.add,
+                )
+                nc.vector.tensor_reduce(
+                    out=neg_max[:, t : t + 1], in_=logits[:, t, :], axis=AXIS_X, op=ALU.max, negate=True
+                )
+                nc.scalar.activation(
+                    out=expd[b][:, t, :],
+                    in_=logits[:, t, :],
+                    func=FUNC.Exp,
+                    bias=neg_max[:, t : t + 1],
+                    scale=1.0,
+                    accum_out=exp_sum[b][:, t : t + 1],
+                )
+
+        def normalise_and_transpose(b):
+            inv_sum = work.tile([P, TT], F32)
+            nc.vector.reciprocal(out=inv_sum[:], in_=exp_sum[b][:])
+            attn = work.tile([P, TT, PACK, P], BF16)
+            for t in range(TT):
+                nc.scalar.activation(
+                    out=attn[:, t].rearrange("p c j -> p (c j)"),
+                    in_=expd[b][:, t, :],
+                    func=FUNC.Copy,
+                    scale=inv_sum[:, t : t + 1],
+                )
+            attn_ps[b] = psum.tile([P, TT, PACK, P], BF16, name="attn_ps")
+            for t in range(TT):
+                for c in range(PACK):
+                    nc.tensor.transpose(attn_ps[b][:, t, c, :], attn[:, t, c, :], ident[:])
+
+        def regroup_attention(b):
+            attn_grouped[b] = work.tile([P, TT, P, PACK], BF16, name="attn_grouped", bufs=B, align_bytes=64)
+            nc.scalar.copy(out=attn_grouped[b][:], in_=attn_ps[b][:].rearrange("p t c k -> p t k c"))
+
+        def quantise_attention(b):
+            cols = slice(b * TT * P, (b + 1) * TT * P)
+            nc.vector.quantize_mx(
+                out=attn_codes[:, cols].bitcast(FP8X4),
+                scales=attn_scales[:, cols],
+                in_=attn_grouped[b][:].rearrange("p t k c -> p (t k c)"),
+            )
+
+        def regroup_values(n):
+            cols = slice(n * N_TILE, (n + 1) * N_TILE)
+            val_grouped[n] = work.tile([P, N_TILE, PACK], BF16, name="val_grouped", bufs=N_TILES, align_bytes=64)
+            nc.vector.tensor_copy(
+                out=val_grouped[n][:].rearrange("p (w i) j -> p w j i", i=4),
+                in_=val_raw[:, :, cols].rearrange("p j (w i) -> p w j i", i=4),
+            )
+
+        def quantise_values(n):
+            cols = slice(n * N_TILE, (n + 1) * N_TILE)
+            nc.vector.quantize_mx(
+                out=val_codes[:, cols].bitcast(FP8X4),
+                scales=val_scales[:, cols],
+                in_=val_grouped[n][:].rearrange("p w j -> p (w j)"),
+            )
+
+        def head_mean(b):
+            avg_ps[b] = bank([P, KH, TT, P], F32, "avg_ps")
+            avg_cols = avg_ps[b][:].rearrange("k kh t (sh j) -> k kh t j sh", sh=S_HI)
+            for s_lo in range(S_LO):
+                for kh in range(KH):
+                    nc.tensor.matmul(
+                        avg_cols[:, kh, s_lo % TT, s_lo // TT, :],
+                        lhsT=paw_sb[b][:, s_lo, kh * P : (kh + 1) * P],
+                        rhs=head_mean_sel[:],
+                        start=True,
+                        stop=True,
+                    )
+
+        def log_of_head_mean(b):
+            log_avg[b] = work.tile([P, KH * TT * P], F32, name="log_avg", bufs=AHEAD)
+            nc.scalar.activation(
+                out=log_avg[b][:],
+                in_=avg_ps[b][:].rearrange("k kh t p -> k (kh t p)"),
+                func=FUNC.Ln,
+                bias=eps[:],
+                scale=1.0,
+            )
+
+        def entropy(b):
+            terms = work.tile([P, KH, TT, P], F32)
+            nc.vector.tensor_tensor(
+                out=terms[:].rearrange("k kh t p -> k (kh t p)"),
+                in0=avg_ps[b][:].rearrange("k kh t p -> k (kh t p)"),
+                in1=log_avg[b][:],
+                op=ALU.mult,
+            )
+            ent_ps[b] = psum.tile([P, TT], F32, name="ent_ps")
+            for t in range(TT):
+                for kh in range(KH):
+                    nc.tensor.matmul(
+                        ent_ps[b][:, t : t + 1],
+                        lhsT=terms[:, kh, t, :],
+                        rhs=minus_ones[:],
+                        start=(kh == 0),
+                        stop=(kh == KH - 1),
+                    )
+
+        def gate_exponent(b):
+            x = work.tile([P, TT], F32)
+            nc.vector.tensor_scalar(
+                out=x[:], in0=ent_ps[b][:], scalar1=w1_neg[:], scalar2=bias_neg[:], op0=ALU.mult, op1=ALU.add
+            )
+            two_to_x[b] = work.tile([P, TT], F32, name="two_to_x")
+            nc.gpsimd.tensor_tensor(out=two_to_x[b][:], in0=twos[:], in1=x[:], op=ALU.pow)
+            cap = work.tile([P, TT], F32)
+            nc.vector.tensor_scalar(
+                out=cap[:], in0=ent_ps[b][:], scalar1=TAU_HIGH, scalar2=GATE_CAP, op0=ALU.is_le, op1=ALU.max
+            )
+            limit[b] = work.tile([P, TT], F32, name="limit")
+            nc.vector.scalar_tensor_tensor(
+                out=limit[b][:], in0=ent_ps[b][:], scalar=TAU_LOW, in1=cap[:], op0=ALU.is_ge, op1=ALU.mult
+            )
+
+        def finish_gate(b):
+            denom = work.tile([P, TT], F32)
+            nc.vector.tensor_scalar_add(out=denom[:], in0=two_to_x[b][:], scalar1=1.0)
+            sigmoid = work.tile([P, TT], F32)
+            nc.vector.reciprocal(out=sigmoid[:], in_=denom[:])
+            gate[b] = work.tile([P, TT], F32, name="gate")
+            nc.vector.tensor_tensor(out=gate[b][:], in0=sigmoid[:], in1=limit[b][:], op=ALU.min)
+
+        def products(b, t):
+            toks = slice((b * TT + t) * P, (b * TT + t + 1) * P)
+            for n in range(N_TILES):
+                cols = slice(n * N_TILE, (n + 1) * N_TILE)
+                aux_ps[(b, t, n)] = bank([P, N_TILE], F32, "aux_ps")
+                nc.tensor.matmul_mx(
+                    out=aux_ps[(b, t, n)][:],
+                    lhsT=attn_codes[:, toks].bitcast(FP8X4),
+                    lhsT_scale=attn_scales[:, toks],
+                    rhs=val_codes[:, cols].bitcast(FP8X4),
+                    rhs_scale=val_scales[:, cols],
+                    start=True,
+                    stop=True,
+                )
+
+        def blend_and_store(b, t):
+            if t == 0:
+                mixed[b] = resident.tile([P, TT, H], F32, name="mixed%d" % b, tag="stream", bufs=B)
+            for n in range(N_TILES):
+                cols = slice(n * N_TILE, (n + 1) * N_TILE)
+                nc.vector.scalar_tensor_tensor(
+                    out=mixed[b][:, t, cols],
+                    in0=aux_ps[(b, t, n)][:],
+                    scalar=gate[b][:, t : t + 1],
+                    in1=pao_sb[b][:, t, cols],
+                    op0=ALU.mult,
+                    op1=ALU.add,
+                )
+            nc.sync.dma_start(out=out_view[b, :, t, :], in_=mixed[b][:, t, :])
+
+        def softmax_tail(i):
+            if 0 <= i - 2 < B:
+                regroup_attention(i - 2)
+            if 0 <= i - 1 < B:
+                normalise_and_transpose(i - 1)
+
+        scores(0)
+        scores(1)
+        for i in range(B):
+            if i + 2 < B:
+                scores(i + 2)
+            softmax_tail(i - 1)
+            exponentials(i)
+        for b in range(AHEAD):
+            head_mean(b)
+            log_of_head_mean(b)
+
+        for n in range(N_TILES):
+            regroup_values(n)
+            if n >= 1:
+                quantise_values(n - 1)
+            softmax_tail(B - 1 + n)
+        entropy(0)
+        quantise_values(N_TILES - 1)
+        quantise_attention(0)
+        gate_exponent(0)
+
+        for b in range(B):
+            products(b, 0)
+            if b + 1 < B:
+                entropy(b + 1)
+            finish_gate(b)
+            blend_and_store(b, 0)
+            products(b, 1)
+            if b + 1 < B:
+                gate_exponent(b + 1)
+                quantise_attention(b + 1)
+            if b + AHEAD < B:
+                head_mean(b + AHEAD)
+                log_of_head_mean(b + AHEAD)
+            blend_and_store(b, 1)

@@ -73,11 +73,13 @@ def tile_auxiliarygovernedattention_pa_kernel(
         out_view = out.rearrange("b (p t) h -> b p t h", t=TT)
         paw_sb = []
         pao_sb = []
-        for b in range(B):
-            paw_sb.append(resident.tile([P, S_LO, S], BF16, name="paw%d" % b, tag="stream", bufs=B))
-            nc.sync.dma_start(out=paw_sb[b][:], in_=paw_view[b])
-            pao_sb.append(resident.tile([P, TT, H], BF16, name="pao%d" % b))
-            nc.sync.dma_start(out=pao_sb[b][:], in_=pao_view[b])
+        for b in range(B + 1):
+            if b < B:
+                paw_sb.append(resident.tile([P, S_LO, S], BF16, name="paw%d" % b, tag="stream", bufs=B))
+                nc.sync.dma_start(out=paw_sb[b][:], in_=paw_view[b])
+            if b >= 1:
+                pao_sb.append(resident.tile([P, TT, H], BF16, name="pao%d" % (b - 1)))
+                nc.sync.dma_start(out=pao_sb[b - 1][:], in_=pao_view[b - 1])
 
         ident = const.tile([P, P], BF16)
         make_identity(nc, ident[:])
@@ -164,8 +166,8 @@ def tile_auxiliarygovernedattention_pa_kernel(
         def exponentials(b):
             logits = work.tile([P, TT, NS], F32)
             neg_max = work.tile([P, TT], F32)
-            expd[b] = work.tile([P, TT, NS], F32, name="expd")
-            exp_sum[b] = work.tile([P, TT], F32, name="exp_sum")
+            expd[b] = work.tile([P, TT, NS], F32, name="expd", bufs=B)
+            exp_sum[b] = work.tile([P, TT], F32, name="exp_sum", bufs=B)
             for t in range(TT):
                 nc.vector.scalar_tensor_tensor(
                     out=logits[:, t, :],
@@ -231,10 +233,11 @@ def tile_auxiliarygovernedattention_pa_kernel(
                 in_=val_grouped[n][:].rearrange("p w j -> p (w j)"),
             )
 
-        def head_mean(b):
-            avg_ps[b] = bank([P, KH, TT, P], F32, "avg_ps")
+        def head_mean(b, half):
+            if half == 0:
+                avg_ps[b] = bank([P, KH, TT, P], F32, "avg_ps")
             avg_cols = avg_ps[b][:].rearrange("k kh t (sh j) -> k kh t j sh", sh=S_HI)
-            for s_lo in range(S_LO):
+            for s_lo in range(half * S_LO // 2, (half + 1) * S_LO // 2):
                 for kh in range(KH):
                     nc.tensor.matmul(
                         avg_cols[:, kh, s_lo % TT, s_lo // TT, :],
@@ -312,10 +315,10 @@ def tile_auxiliarygovernedattention_pa_kernel(
                     stop=True,
                 )
 
-        def blend_and_store(b, t):
-            if t == 0:
+        def blend(b, t, n_from, n_to):
+            if t == 0 and n_from == 0:
                 mixed[b] = resident.tile([P, TT, H], F32, name="mixed%d" % b, tag="stream", bufs=B)
-            for n in range(N_TILES):
+            for n in range(n_from, n_to):
                 cols = slice(n * N_TILE, (n + 1) * N_TILE)
                 nc.vector.scalar_tensor_tensor(
                     out=mixed[b][:, t, cols],
@@ -325,46 +328,51 @@ def tile_auxiliarygovernedattention_pa_kernel(
                     op0=ALU.mult,
                     op1=ALU.add,
                 )
-            nc.sync.dma_start(out=out_view[b, :, t, :], in_=mixed[b][:, t, :])
-
-        def softmax_tail(i):
-            if 0 <= i - 2 < B:
-                regroup_attention(i - 2)
-            if 0 <= i - 1 < B:
-                normalise_and_transpose(i - 1)
+            if n_to == N_TILES:
+                nc.sync.dma_start(out=out_view[b, :, t, :], in_=mixed[b][:, t, :])
 
         scores(0)
         scores(1)
         for i in range(B):
             if i + 2 < B:
                 scores(i + 2)
-            softmax_tail(i - 1)
+            if 0 <= i - 3 < AHEAD:
+                regroup_attention(i - 3)
+            if 0 <= i - 2 < AHEAD:
+                normalise_and_transpose(i - 2)
             exponentials(i)
-        for b in range(AHEAD):
-            head_mean(b)
-            log_of_head_mean(b)
+            if 0 <= i - 2 < AHEAD:
+                head_mean(i - 2, 0)
+                head_mean(i - 2, 1)
+        log_of_head_mean(0)
+        regroup_attention(1)
+        log_of_head_mean(1)
 
         for n in range(N_TILES):
             regroup_values(n)
             if n >= 1:
                 quantise_values(n - 1)
-            softmax_tail(B - 1 + n)
         entropy(0)
         quantise_values(N_TILES - 1)
         quantise_attention(0)
         gate_exponent(0)
 
         for b in range(B):
+            finish_gate(b)
             products(b, 0)
+            if b + AHEAD < B:
+                normalise_and_transpose(b + AHEAD)
+                head_mean(b + AHEAD, 0)
+            blend(b, 0, 0, N_TILES)
+            products(b, 1)
             if b + 1 < B:
                 entropy(b + 1)
-            finish_gate(b)
-            blend_and_store(b, 0)
-            products(b, 1)
+            if b + AHEAD < B:
+                regroup_attention(b + AHEAD)
+                head_mean(b + AHEAD, 1)
+                log_of_head_mean(b + AHEAD)
+            blend(b, 1, 0, N_TILES // 2)
             if b + 1 < B:
                 gate_exponent(b + 1)
                 quantise_attention(b + 1)
-            if b + AHEAD < B:
-                head_mean(b + AHEAD)
-                log_of_head_mean(b + AHEAD)
-            blend_and_store(b, 1)
+            blend(b, 1, N_TILES // 2, N_TILES)

@@ -320,14 +320,23 @@ def tile_auxiliarygovernedattention_pa_kernel(
                 mixed[b] = resident.tile([P, TT, H], F32, name="mixed%d" % b, tag="stream", bufs=B)
             for n in range(n_from, n_to):
                 cols = slice(n * N_TILE, (n + 1) * N_TILE)
-                nc.vector.scalar_tensor_tensor(
-                    out=mixed[b][:, t, cols],
-                    in0=aux_ps[(b, t, n)][:],
-                    scalar=gate[b][:, t : t + 1],
-                    in1=pao_sb[b][:, t, cols],
-                    op0=ALU.mult,
-                    op1=ALU.add,
-                )
+                if n == 0:
+                    gated = work.tile([P, N_TILE], F32)
+                    nc.scalar.activation(
+                        out=gated[:], in_=aux_ps[(b, t, n)][:], func=FUNC.Copy, scale=gate[b][:, t : t + 1]
+                    )
+                    nc.gpsimd.tensor_tensor(
+                        out=mixed[b][:, t, cols], in0=gated[:], in1=pao_sb[b][:, t, cols], op=ALU.add
+                    )
+                else:
+                    nc.vector.scalar_tensor_tensor(
+                        out=mixed[b][:, t, cols],
+                        in0=aux_ps[(b, t, n)][:],
+                        scalar=gate[b][:, t : t + 1],
+                        in1=pao_sb[b][:, t, cols],
+                        op0=ALU.mult,
+                        op1=ALU.add,
+                    )
             if n_to == N_TILES:
                 nc.sync.dma_start(out=out_view[b, :, t, :], in_=mixed[b][:, t, :])
 

@@ -27,6 +27,7 @@ TAU_HIGH = 2.0
 GATE_CAP = 0.8
 EPS = 1e-10
 AHEAD = 2
+PIECES = 8
 LOG2_E = 1.0 / math.log(2.0)
 
 FLOPS = 2 * B * S * NS * (D + H)
@@ -138,8 +139,10 @@ def tile_auxiliarygovernedattention_pa_kernel(
         val_scales = resident.tile([P, H], U8, align_bytes=64)
 
         score_ps = {}
-        expd = {}
+        logit = {}
+        neg_max = {}
         exp_sum = {}
+        attn = {}
         attn_ps = {}
         attn_grouped = {}
         val_grouped = {}
@@ -163,14 +166,12 @@ def tile_auxiliarygovernedattention_pa_kernel(
                     stop=True,
                 )
 
-        def exponentials(b):
-            logits = work.tile([P, TT, NS], F32)
-            neg_max = work.tile([P, TT], F32)
-            expd[b] = work.tile([P, TT, NS], F32, name="expd", bufs=B)
-            exp_sum[b] = work.tile([P, TT], F32, name="exp_sum", bufs=B)
+        def logits(b):
+            logit[b] = work.tile([P, TT, NS], F32, name="logit", bufs=B)
+            neg_max[b] = work.tile([P, TT], F32, name="neg_max", bufs=B)
             for t in range(TT):
                 nc.vector.scalar_tensor_tensor(
-                    out=logits[:, t, :],
+                    out=logit[b][:, t, :],
                     in0=score_ps[(b, t)][:],
                     scalar=1.0 / math.sqrt(D),
                     in1=log_rel[:].rearrange("p c j -> p (c j)"),
@@ -178,32 +179,38 @@ def tile_auxiliarygovernedattention_pa_kernel(
                     op1=ALU.add,
                 )
                 nc.vector.tensor_reduce(
-                    out=neg_max[:, t : t + 1], in_=logits[:, t, :], axis=AXIS_X, op=ALU.max, negate=True
+                    out=neg_max[b][:, t : t + 1], in_=logit[b][:, t, :], axis=AXIS_X, op=ALU.max, negate=True
                 )
+
+        def exponentials(b):
+            exp_sum[b] = work.tile([P, TT], F32, name="exp_sum", bufs=B)
+            for t in range(TT):
                 nc.scalar.activation(
-                    out=expd[b][:, t, :],
-                    in_=logits[:, t, :],
+                    out=logit[b][:, t, :],
+                    in_=logit[b][:, t, :],
                     func=FUNC.Exp,
-                    bias=neg_max[:, t : t + 1],
+                    bias=neg_max[b][:, t : t + 1],
                     scale=1.0,
                     accum_out=exp_sum[b][:, t : t + 1],
                 )
 
-        def normalise_and_transpose(b):
+        def normalise(b):
             inv_sum = work.tile([P, TT], F32)
             nc.vector.reciprocal(out=inv_sum[:], in_=exp_sum[b][:])
-            attn = work.tile([P, TT, PACK, P], BF16)
+            attn[b] = work.tile([P, TT, PACK, P], BF16, name="attn")
             for t in range(TT):
                 nc.scalar.activation(
-                    out=attn[:, t].rearrange("p c j -> p (c j)"),
-                    in_=expd[b][:, t, :],
+                    out=attn[b][:, t].rearrange("p c j -> p (c j)"),
+                    in_=logit[b][:, t, :],
                     func=FUNC.Copy,
                     scale=inv_sum[:, t : t + 1],
                 )
+
+        def transpose_attention(b):
             attn_ps[b] = psum.tile([P, TT, PACK, P], BF16, name="attn_ps")
             for t in range(TT):
                 for c in range(PACK):
-                    nc.tensor.transpose(attn_ps[b][:, t, c, :], attn[:, t, c, :], ident[:])
+                    nc.tensor.transpose(attn_ps[b][:, t, c, :], attn[b][:, t, c, :], ident[:])
 
         def regroup_attention(b):
             attn_grouped[b] = work.tile([P, TT, P, PACK], BF16, name="attn_grouped", bufs=B, align_bytes=64)
@@ -233,11 +240,11 @@ def tile_auxiliarygovernedattention_pa_kernel(
                 in_=val_grouped[n][:].rearrange("p w j -> p (w j)"),
             )
 
-        def head_mean(b, half):
-            if half == 0:
+        def head_mean(b, piece):
+            if piece == 0:
                 avg_ps[b] = bank([P, KH, TT, P], F32, "avg_ps")
             avg_cols = avg_ps[b][:].rearrange("k kh t (sh j) -> k kh t j sh", sh=S_HI)
-            for s_lo in range(half * S_LO // 2, (half + 1) * S_LO // 2):
+            for s_lo in range(piece * S_LO // PIECES, (piece + 1) * S_LO // PIECES):
                 for kh in range(KH):
                     nc.tensor.matmul(
                         avg_cols[:, kh, s_lo % TT, s_lo // TT, :],
@@ -300,7 +307,7 @@ def tile_auxiliarygovernedattention_pa_kernel(
             gate[b] = work.tile([P, TT], F32, name="gate")
             nc.vector.tensor_tensor(out=gate[b][:], in0=sigmoid[:], in1=limit[b][:], op=ALU.min)
 
-        def products(b, t):
+        def products(b, t, averaged, first_piece):
             toks = slice((b * TT + t) * P, (b * TT + t + 1) * P)
             for n in range(N_TILES):
                 cols = slice(n * N_TILE, (n + 1) * N_TILE)
@@ -314,29 +321,22 @@ def tile_auxiliarygovernedattention_pa_kernel(
                     start=True,
                     stop=True,
                 )
+                if averaged < B:
+                    head_mean(averaged, first_piece + n)
 
         def blend(b, t, n_from, n_to):
             if t == 0 and n_from == 0:
                 mixed[b] = resident.tile([P, TT, H], F32, name="mixed%d" % b, tag="stream", bufs=B)
             for n in range(n_from, n_to):
                 cols = slice(n * N_TILE, (n + 1) * N_TILE)
-                if n == 0:
-                    gated = work.tile([P, N_TILE], F32)
-                    nc.scalar.activation(
-                        out=gated[:], in_=aux_ps[(b, t, n)][:], func=FUNC.Copy, scale=gate[b][:, t : t + 1]
-                    )
-                    nc.gpsimd.tensor_tensor(
-                        out=mixed[b][:, t, cols], in0=gated[:], in1=pao_sb[b][:, t, cols], op=ALU.add
-                    )
-                else:
-                    nc.vector.scalar_tensor_tensor(
-                        out=mixed[b][:, t, cols],
-                        in0=aux_ps[(b, t, n)][:],
-                        scalar=gate[b][:, t : t + 1],
-                        in1=pao_sb[b][:, t, cols],
-                        op0=ALU.mult,
-                        op1=ALU.add,
-                    )
+                nc.vector.scalar_tensor_tensor(
+                    out=mixed[b][:, t, cols],
+                    in0=aux_ps[(b, t, n)][:],
+                    scalar=gate[b][:, t : t + 1],
+                    in1=pao_sb[b][:, t, cols],
+                    op0=ALU.mult,
+                    op1=ALU.add,
+                )
             if n_to == N_TILES:
                 nc.sync.dma_start(out=out_view[b, :, t, :], in_=mixed[b][:, t, :])
 
@@ -348,40 +348,44 @@ def tile_auxiliarygovernedattention_pa_kernel(
             if 0 <= i - 3 < AHEAD:
                 regroup_attention(i - 3)
             if 0 <= i - 2 < AHEAD:
-                normalise_and_transpose(i - 2)
-            exponentials(i)
-            if 0 <= i - 2 < AHEAD:
-                head_mean(i - 2, 0)
-                head_mean(i - 2, 1)
-        log_of_head_mean(0)
-        regroup_attention(1)
-        log_of_head_mean(1)
+                for piece in range(PIECES):
+                    head_mean(i - 2, piece)
+                normalise(i - 2)
+                transpose_attention(i - 2)
+                log_of_head_mean(i - 2)
+            logits(i)
+            if i < AHEAD:
+                exponentials(i)
+        regroup_attention(AHEAD - 1)
+        for b in range(AHEAD, B):
+            exponentials(b)
 
+        entropy(0)
         for n in range(N_TILES):
             regroup_values(n)
             if n >= 1:
                 quantise_values(n - 1)
-        entropy(0)
+        gate_exponent(0)
         quantise_values(N_TILES - 1)
         quantise_attention(0)
-        gate_exponent(0)
+        products(0, 0, B, 0)
 
         for b in range(B):
-            finish_gate(b)
-            products(b, 0)
-            if b + AHEAD < B:
-                normalise_and_transpose(b + AHEAD)
-                head_mean(b + AHEAD, 0)
-            blend(b, 0, 0, N_TILES)
-            products(b, 1)
             if b + 1 < B:
                 entropy(b + 1)
+            finish_gate(b)
+            products(b, 1, b + AHEAD, 0)
+            blend(b, 0, 0, N_TILES)
             if b + AHEAD < B:
-                regroup_attention(b + AHEAD)
-                head_mean(b + AHEAD, 1)
+                for piece in range(N_TILES, PIECES):
+                    head_mean(b + AHEAD, piece)
                 log_of_head_mean(b + AHEAD)
-            blend(b, 1, 0, N_TILES // 2)
+                normalise(b + AHEAD)
             if b + 1 < B:
                 gate_exponent(b + 1)
                 quantise_attention(b + 1)
-            blend(b, 1, N_TILES // 2, N_TILES)
+                products(b + 1, 0, B, 0)
+            if b + AHEAD < B:
+                transpose_attention(b + AHEAD)
+                regroup_attention(b + AHEAD)
+            blend(b, 1, 0, N_TILES)

@@ -149,7 +149,10 @@ def tile_auxiliarygovernedattention_pa_kernel(
         avg_ps = {}
         log_avg = {}
         ent_ps = {}
+        cap = {}
         limit = {}
+        denom = {}
+        sigmoid = {}
         two_to_x = {}
         gate = {}
         aux_ps = {}
@@ -178,6 +181,7 @@ def tile_auxiliarygovernedattention_pa_kernel(
                     op0=ALU.mult,
                     op1=ALU.add,
                 )
+            for t in range(TT):
                 nc.vector.tensor_reduce(
                     out=neg_max[b][:, t : t + 1], in_=logit[b][:, t, :], axis=AXIS_X, op=ALU.max, negate=True
                 )
@@ -283,29 +287,32 @@ def tile_auxiliarygovernedattention_pa_kernel(
                         stop=(kh == KH - 1),
                     )
 
-        def gate_exponent(b):
-            x = work.tile([P, TT], F32)
-            nc.vector.tensor_scalar(
-                out=x[:], in0=ent_ps[b][:], scalar1=w1_neg[:], scalar2=bias_neg[:], op0=ALU.mult, op1=ALU.add
-            )
-            two_to_x[b] = work.tile([P, TT], F32, name="two_to_x")
-            nc.gpsimd.tensor_tensor(out=two_to_x[b][:], in0=twos[:], in1=x[:], op=ALU.pow)
-            cap = work.tile([P, TT], F32)
-            nc.vector.tensor_scalar(
-                out=cap[:], in0=ent_ps[b][:], scalar1=TAU_HIGH, scalar2=GATE_CAP, op0=ALU.is_le, op1=ALU.max
-            )
-            limit[b] = work.tile([P, TT], F32, name="limit")
-            nc.vector.scalar_tensor_tensor(
-                out=limit[b][:], in0=ent_ps[b][:], scalar=TAU_LOW, in1=cap[:], op0=ALU.is_ge, op1=ALU.mult
-            )
-
-        def finish_gate(b):
-            denom = work.tile([P, TT], F32)
-            nc.vector.tensor_scalar_add(out=denom[:], in0=two_to_x[b][:], scalar1=1.0)
-            sigmoid = work.tile([P, TT], F32)
-            nc.vector.reciprocal(out=sigmoid[:], in_=denom[:])
-            gate[b] = work.tile([P, TT], F32, name="gate")
-            nc.vector.tensor_tensor(out=gate[b][:], in0=sigmoid[:], in1=limit[b][:], op=ALU.min)
+        def gate_step(b, step):
+            if step == 0:
+                x = work.tile([P, TT], F32)
+                nc.vector.tensor_scalar(
+                    out=x[:], in0=ent_ps[b][:], scalar1=w1_neg[:], scalar2=bias_neg[:], op0=ALU.mult, op1=ALU.add
+                )
+                two_to_x[b] = work.tile([P, TT], F32, name="two_to_x")
+                nc.gpsimd.tensor_tensor(out=two_to_x[b][:], in0=twos[:], in1=x[:], op=ALU.pow)
+                cap[b] = work.tile([P, TT], F32, name="cap")
+                nc.vector.tensor_scalar(
+                    out=cap[b][:], in0=ent_ps[b][:], scalar1=TAU_HIGH, scalar2=GATE_CAP, op0=ALU.is_le, op1=ALU.max
+                )
+            elif step == 1:
+                limit[b] = work.tile([P, TT], F32, name="limit")
+                nc.vector.scalar_tensor_tensor(
+                    out=limit[b][:], in0=ent_ps[b][:], scalar=TAU_LOW, in1=cap[b][:], op0=ALU.is_ge, op1=ALU.mult
+                )
+            elif step == 2:
+                denom[b] = work.tile([P, TT], F32, name="denom")
+                nc.vector.tensor_scalar_add(out=denom[b][:], in0=two_to_x[b][:], scalar1=1.0)
+            elif step == 3:
+                sigmoid[b] = work.tile([P, TT], F32, name="sigmoid")
+                nc.vector.reciprocal(out=sigmoid[b][:], in_=denom[b][:])
+            else:
+                gate[b] = work.tile([P, TT], F32, name="gate")
+                nc.vector.tensor_tensor(out=gate[b][:], in0=sigmoid[b][:], in1=limit[b][:], op=ALU.min)
 
         def products(b, t, averaged, first_piece):
             toks = slice((b * TT + t) * P, (b * TT + t + 1) * P)
@@ -365,27 +372,37 @@ def tile_auxiliarygovernedattention_pa_kernel(
             regroup_values(n)
             if n >= 1:
                 quantise_values(n - 1)
-        gate_exponent(0)
+                gate_step(0, n - 1)
         quantise_values(N_TILES - 1)
+        gate_step(0, 3)
         quantise_attention(0)
+        gate_step(0, 4)
         products(0, 0, B, 0)
 
         for b in range(B):
-            if b + 1 < B:
+            more = b + 1 < B
+            if more:
                 entropy(b + 1)
-            finish_gate(b)
             products(b, 1, b + AHEAD, 0)
-            blend(b, 0, 0, N_TILES)
+            blend(b, 0, 0, 2)
+            if more:
+                gate_step(b + 1, 0)
+            blend(b, 0, 2, 3)
+            if more:
+                gate_step(b + 1, 1)
+            blend(b, 0, 3, N_TILES)
             if b + AHEAD < B:
                 for piece in range(N_TILES, PIECES):
                     head_mean(b + AHEAD, piece)
                 log_of_head_mean(b + AHEAD)
                 normalise(b + AHEAD)
-            if b + 1 < B:
-                gate_exponent(b + 1)
+            if more:
                 quantise_attention(b + 1)
                 products(b + 1, 0, B, 0)
             if b + AHEAD < B:
                 transpose_attention(b + AHEAD)
                 regroup_attention(b + AHEAD)
-            blend(b, 1, 0, N_TILES)
+            for n in range(N_TILES):
+                blend(b, 1, n, n + 1)
+                if more and n + 2 <= 4:
+                    gate_step(b + 1, n + 2)

@@ -29,6 +29,8 @@ EPS = 1e-10
 AHEAD = 2
 PIECES = 8
 LOG2_E = 1.0 / math.log(2.0)
+VALUES_ON_GPSIMD = (0, 1, 2)
+VALUES_ON_SCALAR = ()
 
 FLOPS = 2 * B * S * NS * (D + H)
 
@@ -54,21 +56,24 @@ def tile_auxiliarygovernedattention_pa_kernel(
         psum = ctx.enter_context(tc.psum_pool(name="psum", bufs=1))
 
         def bank(shape, dtype, name):
-            return psum.tile(shape, dtype, name=name, tag="bank", bufs=6)
+            return psum.tile(shape, dtype, name=name, tag="bank", bufs=4)
 
         rel_rows = const.tile([P, NS], BF16)
         nc.vector.memset(rel_rows[:], 0.0)
         keys_sb = resident.tile([P, PACK, D], BF16)
         nc.sync.dma_start(out=keys_sb[:], in_=aux_keys.rearrange("(p c) d -> p c d", c=PACK))
+        nc.sync.dma_start(out=rel_rows[0:1, :], in_=reliability.rearrange("(o n) -> o n", o=1))
         q_sb = resident.tile([P, B, TT, D], BF16)
         nc.sync.dma_start(out=q_sb[:], in_=query.rearrange("b (p t) d -> p b t d", t=TT))
-        nc.sync.dma_start(out=rel_rows[0:1, :], in_=reliability.rearrange("(o n) -> o n", o=1))
         w1_bf = const.tile([P, 1], BF16)
         bias_bf = const.tile([P, 1], BF16)
         nc.sync.dma_start(out=w1_bf[:], in_=gate_w1.partition_broadcast(P))
         nc.sync.dma_start(out=bias_bf[:], in_=gate_bias.partition_broadcast(P))
         val_raw = resident.tile([P, PACK, H], BF16)
-        nc.sync.dma_start(out=val_raw[:], in_=aux_values.rearrange("(p j) w -> p j w", j=PACK))
+        val_view = aux_values.rearrange("(p j) w -> p j w", j=PACK)
+        for half in range(2):
+            cols = slice(half * H // 2, (half + 1) * H // 2)
+            nc.sync.dma_start(out=val_raw[:, :, cols], in_=val_view[:, :, cols])
         paw_view = primary_attention_weights.rearrange("b h (sh sl) k -> b (h sh) sl k", sh=S_HI)
         pao_view = primary_attention_output.rearrange("b (p t) h -> b p t h", t=TT)
         out_view = out.rearrange("b (p t) h -> b p t h", t=TT)
@@ -77,7 +82,9 @@ def tile_auxiliarygovernedattention_pa_kernel(
         for b in range(B + 1):
             if b < B:
                 paw_sb.append(resident.tile([P, S_LO, S], BF16, name="paw%d" % b, tag="stream", bufs=B))
-                nc.sync.dma_start(out=paw_sb[b][:], in_=paw_view[b])
+                for half in range(2):
+                    rows = slice(half * S_LO // 2, (half + 1) * S_LO // 2)
+                    nc.sync.dma_start(out=paw_sb[b][:, rows, :], in_=paw_view[b][:, rows, :])
             if b >= 1:
                 pao_sb.append(resident.tile([P, TT, H], BF16, name="pao%d" % (b - 1)))
                 nc.sync.dma_start(out=pao_sb[b - 1][:], in_=pao_view[b - 1])
@@ -115,13 +122,6 @@ def tile_auxiliarygovernedattention_pa_kernel(
             nc.tensor.transpose(keys_ps[:, c, :], keys_sb[:, c, :], ident[:])
         keys_t = resident.tile([P, PACK, P], BF16)
         nc.vector.tensor_copy(out=keys_t[:], in_=keys_ps[:])
-        q_ps = bank([P, B * TT, P], BF16, "q_ps")
-        for b in range(B):
-            for t in range(TT):
-                nc.tensor.transpose(q_ps[:, b * TT + t, :], q_sb[:, b, t, :], ident[:])
-        q_t = resident.tile([P, B * TT, P], BF16)
-        nc.vector.tensor_copy(out=q_t[:], in_=q_ps[:])
-
         rel_ps = bank([P, NS], F32, "rel_ps")
         nc.tensor.matmul(rel_ps[:], lhsT=ones[:], rhs=rel_rows[:], start=True, stop=True)
         log_rel = resident.tile([P, PACK, P], F32)
@@ -132,6 +132,12 @@ def tile_auxiliarygovernedattention_pa_kernel(
             bias=eps[:],
             scale=1.0,
         )
+        q_ps = bank([P, B * TT, P], BF16, "q_ps")
+        for b in range(B):
+            for t in range(TT):
+                nc.tensor.transpose(q_ps[:, b * TT + t, :], q_sb[:, b, t, :], ident[:])
+        q_t = resident.tile([P, B * TT, P], BF16)
+        nc.vector.tensor_copy(out=q_t[:], in_=q_ps[:])
 
         attn_codes = resident.tile([P, B * TT * P], U32, align_bytes=64)
         attn_scales = resident.tile([P, B * TT * P], U8, align_bytes=64)
@@ -142,12 +148,14 @@ def tile_auxiliarygovernedattention_pa_kernel(
         logit = {}
         neg_max = {}
         exp_sum = {}
+        inv_sum = {}
         attn = {}
         attn_ps = {}
         attn_grouped = {}
         val_grouped = {}
         avg_ps = {}
         log_avg = {}
+        terms = {}
         ent_ps = {}
         cap = {}
         limit = {}
@@ -171,7 +179,6 @@ def tile_auxiliarygovernedattention_pa_kernel(
 
         def logits(b):
             logit[b] = work.tile([P, TT, NS], F32, name="logit", bufs=B)
-            neg_max[b] = work.tile([P, TT], F32, name="neg_max", bufs=B)
             for t in range(TT):
                 nc.vector.scalar_tensor_tensor(
                     out=logit[b][:, t, :],
@@ -181,6 +188,9 @@ def tile_auxiliarygovernedattention_pa_kernel(
                     op0=ALU.mult,
                     op1=ALU.add,
                 )
+
+        def maxima(b):
+            neg_max[b] = work.tile([P, TT], F32, name="neg_max", bufs=B)
             for t in range(TT):
                 nc.vector.tensor_reduce(
                     out=neg_max[b][:, t : t + 1], in_=logit[b][:, t, :], axis=AXIS_X, op=ALU.max, negate=True
@@ -198,16 +208,18 @@ def tile_auxiliarygovernedattention_pa_kernel(
                     accum_out=exp_sum[b][:, t : t + 1],
                 )
 
+        def invert_sums(b):
+            inv_sum[b] = work.tile([P, TT], F32, name="inv_sum", bufs=B)
+            nc.vector.reciprocal(out=inv_sum[b][:], in_=exp_sum[b][:])
+
         def normalise(b):
-            inv_sum = work.tile([P, TT], F32)
-            nc.vector.reciprocal(out=inv_sum[:], in_=exp_sum[b][:])
-            attn[b] = work.tile([P, TT, PACK, P], BF16, name="attn")
+            attn[b] = work.tile([P, TT, PACK, P], BF16, name="attn", bufs=B)
             for t in range(TT):
                 nc.scalar.activation(
                     out=attn[b][:, t].rearrange("p c j -> p (c j)"),
                     in_=logit[b][:, t, :],
                     func=FUNC.Copy,
-                    scale=inv_sum[:, t : t + 1],
+                    scale=inv_sum[b][:, t : t + 1],
                 )
 
         def transpose_attention(b):
@@ -231,10 +243,22 @@ def tile_auxiliarygovernedattention_pa_kernel(
         def regroup_values(n):
             cols = slice(n * N_TILE, (n + 1) * N_TILE)
             val_grouped[n] = work.tile([P, N_TILE, PACK], BF16, name="val_grouped", bufs=N_TILES, align_bytes=64)
-            nc.vector.tensor_copy(
-                out=val_grouped[n][:].rearrange("p (w i) j -> p w j i", i=4),
-                in_=val_raw[:, :, cols].rearrange("p j (w i) -> p w j i", i=4),
-            )
+            if n in VALUES_ON_GPSIMD:
+                nc.gpsimd.tensor_scalar(
+                    out=val_grouped[n][:],
+                    in0=val_raw[:, :, cols].rearrange("p j w -> p w j"),
+                    scalar1=1.0,
+                    scalar2=0.0,
+                    op0=ALU.mult,
+                    op1=ALU.add,
+                )
+            elif n in VALUES_ON_SCALAR:
+                nc.scalar.copy(out=val_grouped[n][:], in_=val_raw[:, :, cols].rearrange("p j w -> p w j"))
+            else:
+                nc.vector.tensor_copy(
+                    out=val_grouped[n][:].rearrange("p (w i) j -> p w j i", i=4),
+                    in_=val_raw[:, :, cols].rearrange("p j (w i) -> p w j i", i=4),
+                )
 
         def quantise_values(n):
             cols = slice(n * N_TILE, (n + 1) * N_TILE)
@@ -246,7 +270,7 @@ def tile_auxiliarygovernedattention_pa_kernel(
 
         def head_mean(b, piece):
             if piece == 0:
-                avg_ps[b] = bank([P, KH, TT, P], F32, "avg_ps")
+                avg_ps[b] = psum.tile([P, KH, TT, P], F32, name="avg_ps", bufs=2)
             avg_cols = avg_ps[b][:].rearrange("k kh t (sh j) -> k kh t j sh", sh=S_HI)
             for s_lo in range(piece * S_LO // PIECES, (piece + 1) * S_LO // PIECES):
                 for kh in range(KH):
@@ -268,20 +292,22 @@ def tile_auxiliarygovernedattention_pa_kernel(
                 scale=1.0,
             )
 
-        def entropy(b):
-            terms = work.tile([P, KH, TT, P], F32)
+        def entropy_terms(b):
+            terms[b] = work.tile([P, KH, TT, P], F32, name="terms")
             nc.vector.tensor_tensor(
-                out=terms[:].rearrange("k kh t p -> k (kh t p)"),
+                out=terms[b][:].rearrange("k kh t p -> k (kh t p)"),
                 in0=avg_ps[b][:].rearrange("k kh t p -> k (kh t p)"),
                 in1=log_avg[b][:],
                 op=ALU.mult,
             )
+
+        def entropy(b):
             ent_ps[b] = psum.tile([P, TT], F32, name="ent_ps")
             for t in range(TT):
                 for kh in range(KH):
                     nc.tensor.matmul(
                         ent_ps[b][:, t : t + 1],
-                        lhsT=terms[:, kh, t, :],
+                        lhsT=terms[b][:, kh, t, :],
                         rhs=minus_ones[:],
                         start=(kh == 0),
                         stop=(kh == KH - 1),
@@ -314,7 +340,7 @@ def tile_auxiliarygovernedattention_pa_kernel(
                 gate[b] = work.tile([P, TT], F32, name="gate")
                 nc.vector.tensor_tensor(out=gate[b][:], in0=sigmoid[b][:], in1=limit[b][:], op=ALU.min)
 
-        def products(b, t, averaged, first_piece):
+        def products(b, t, averaged=B, first_piece=0, per_pass=1, entropy_after=N_TILES):
             toks = slice((b * TT + t) * P, (b * TT + t + 1) * P)
             for n in range(N_TILES):
                 cols = slice(n * N_TILE, (n + 1) * N_TILE)
@@ -329,7 +355,10 @@ def tile_auxiliarygovernedattention_pa_kernel(
                     stop=True,
                 )
                 if averaged < B:
-                    head_mean(averaged, first_piece + n)
+                    for piece in range(first_piece + n * per_pass, first_piece + (n + 1) * per_pass):
+                        head_mean(averaged, piece)
+                if n == entropy_after and b + 1 < B:
+                    entropy(b + 1)
 
         def blend(b, t, n_from, n_to):
             if t == 0 and n_from == 0:
@@ -344,65 +373,86 @@ def tile_auxiliarygovernedattention_pa_kernel(
                     op0=ALU.mult,
                     op1=ALU.add,
                 )
-            if n_to == N_TILES:
+            if (b, t) == (B - 1, TT - 1):
+                cols = slice(n_from * N_TILE, n_to * N_TILE)
+                nc.sync.dma_start(out=out_view[b, :, t, cols], in_=mixed[b][:, t, cols])
+            elif n_to == N_TILES:
                 nc.sync.dma_start(out=out_view[b, :, t, :], in_=mixed[b][:, t, :])
 
+        for n in VALUES_ON_GPSIMD:
+            regroup_values(n)
         scores(0)
         scores(1)
-        for i in range(B):
-            if i + 2 < B:
-                scores(i + 2)
-            if 0 <= i - 3 < AHEAD:
-                regroup_attention(i - 3)
-            if 0 <= i - 2 < AHEAD:
-                for piece in range(PIECES):
-                    head_mean(i - 2, piece)
-                normalise(i - 2)
-                transpose_attention(i - 2)
-                log_of_head_mean(i - 2)
-            logits(i)
-            if i < AHEAD:
-                exponentials(i)
-        regroup_attention(AHEAD - 1)
-        for b in range(AHEAD, B):
-            exponentials(b)
-
+        logits(0)
+        maxima(0)
+        exponentials(0)
+        scores(2)
+        logits(1)
+        invert_sums(0)
+        normalise(0)
+        maxima(1)
+        exponentials(1)
+        scores(3)
+        transpose_attention(0)
+        logits(2)
+        invert_sums(1)
+        normalise(1)
+        maxima(2)
+        exponentials(2)
+        for piece in range(PIECES):
+            head_mean(0, piece)
+        logits(3)
+        invert_sums(2)
+        maxima(3)
+        exponentials(3)
+        for piece in range(PIECES):
+            head_mean(1, piece)
+        log_of_head_mean(0)
+        regroup_attention(0)
+        regroup_values(3)
+        invert_sums(3)
+        quantise_values(0)
+        quantise_values(1)
+        entropy_terms(0)
         entropy(0)
-        for n in range(N_TILES):
-            regroup_values(n)
-            if n >= 1:
-                quantise_values(n - 1)
-                gate_step(0, n - 1)
-        quantise_values(N_TILES - 1)
-        gate_step(0, 3)
+        quantise_values(2)
         quantise_attention(0)
+        gate_step(0, 0)
+        quantise_values(3)
+        transpose_attention(1)
+        products(0, 0)
+        normalise(2)
+        regroup_attention(1)
+        log_of_head_mean(1)
+        normalise(3)
+        transpose_attention(2)
+        regroup_attention(2)
+        gate_step(0, 1)
+        gate_step(0, 2)
+        gate_step(0, 3)
         gate_step(0, 4)
-        products(0, 0, B, 0)
 
         for b in range(B):
             more = b + 1 < B
-            if more:
-                entropy(b + 1)
-            products(b, 1, b + AHEAD, 0)
             blend(b, 0, 0, 2)
             if more:
-                gate_step(b + 1, 0)
-            blend(b, 0, 2, 3)
-            if more:
-                gate_step(b + 1, 1)
-            blend(b, 0, 3, N_TILES)
-            if b + AHEAD < B:
-                for piece in range(N_TILES, PIECES):
-                    head_mean(b + AHEAD, piece)
-                log_of_head_mean(b + AHEAD)
-                normalise(b + AHEAD)
+                entropy_terms(b + 1)
+            products(b, 1, b + 2, 0, 1, 1)
+            blend(b, 0, 2, N_TILES)
             if more:
                 quantise_attention(b + 1)
-                products(b + 1, 0, B, 0)
-            if b + AHEAD < B:
-                transpose_attention(b + AHEAD)
-                regroup_attention(b + AHEAD)
-            for n in range(N_TILES):
+            if b == 0:
+                transpose_attention(3)
+                regroup_attention(3)
+            if more:
+                products(b + 1, 0, b + 2, 4, 1)
+            if b + 2 < B:
+                log_of_head_mean(b + 2)
+            blend(b, 1, 0, 1)
+            for n in range(1, N_TILES):
+                if more:
+                    gate_step(b + 1, n - 1)
                 blend(b, 1, n, n + 1)
-                if more and n + 2 <= 4:
-                    gate_step(b + 1, n + 2)
+            if more:
+                gate_step(b + 1, 3)
+                gate_step(b + 1, 4)

@@ -212,15 +212,15 @@ def tile_auxiliarygovernedattention_pa_kernel(
             inv_sum[b] = work.tile([P, TT], F32, name="inv_sum", bufs=B)
             nc.vector.reciprocal(out=inv_sum[b][:], in_=exp_sum[b][:])
 
-        def normalise(b):
-            attn[b] = work.tile([P, TT, PACK, P], BF16, name="attn", bufs=B)
-            for t in range(TT):
-                nc.scalar.activation(
-                    out=attn[b][:, t].rearrange("p c j -> p (c j)"),
-                    in_=logit[b][:, t, :],
-                    func=FUNC.Copy,
-                    scale=inv_sum[b][:, t : t + 1],
-                )
+        def normalise(b, t):
+            if t == 0:
+                attn[b] = work.tile([P, TT, PACK, P], BF16, name="attn", bufs=B)
+            nc.scalar.activation(
+                out=attn[b][:, t].rearrange("p c j -> p (c j)"),
+                in_=logit[b][:, t, :],
+                func=FUNC.Copy,
+                scale=inv_sum[b][:, t : t + 1],
+            )
 
         def transpose_attention(b):
             attn_ps[b] = psum.tile([P, TT, PACK, P], BF16, name="attn_ps")
@@ -389,18 +389,19 @@ def tile_auxiliarygovernedattention_pa_kernel(
         scores(2)
         logits(1)
         invert_sums(0)
-        normalise(0)
+        normalise(0, 0)
         maxima(1)
         exponentials(1)
+        normalise(0, 1)
         scores(3)
-        transpose_attention(0)
         logits(2)
         invert_sums(1)
-        normalise(1)
         maxima(2)
         exponentials(2)
+        normalise(1, 0)
         for piece in range(PIECES):
             head_mean(0, piece)
+        transpose_attention(0)
         logits(3)
         invert_sums(2)
         maxima(3)
@@ -409,6 +410,8 @@ def tile_auxiliarygovernedattention_pa_kernel(
             head_mean(1, piece)
         log_of_head_mean(0)
         regroup_attention(0)
+        log_of_head_mean(1)
+        normalise(1, 1)
         regroup_values(3)
         invert_sums(3)
         quantise_values(0)
@@ -419,14 +422,11 @@ def tile_auxiliarygovernedattention_pa_kernel(
         quantise_attention(0)
         gate_step(0, 0)
         quantise_values(3)
-        transpose_attention(1)
         products(0, 0)
-        normalise(2)
+        transpose_attention(1)
         regroup_attention(1)
-        log_of_head_mean(1)
-        normalise(3)
-        transpose_attention(2)
-        regroup_attention(2)
+        normalise(2, 0)
+        normalise(2, 1)
         gate_step(0, 1)
         gate_step(0, 2)
         gate_step(0, 3)
@@ -434,25 +434,30 @@ def tile_auxiliarygovernedattention_pa_kernel(
 
         for b in range(B):
             more = b + 1 < B
-            blend(b, 0, 0, 2)
-            if more:
-                entropy_terms(b + 1)
-            products(b, 1, b + 2, 0, 1, 1)
-            blend(b, 0, 2, N_TILES)
+            products(b, 1, b + 2, 0)
+            blend(b, 0, 0, N_TILES)
             if more:
                 quantise_attention(b + 1)
+                entropy_terms(b + 1)
+                entropy(b + 1)
+            if b + 2 < B:
+                transpose_attention(b + 2)
+                regroup_attention(b + 2)
             if b == 0:
-                transpose_attention(3)
-                regroup_attention(3)
+                normalise(3, 0)
+                normalise(3, 1)
             if more:
-                products(b + 1, 0, b + 2, 4, 1)
+                products(b + 1, 0, b + 2, N_TILES)
             if b + 2 < B:
                 log_of_head_mean(b + 2)
-            blend(b, 1, 0, 1)
-            for n in range(1, N_TILES):
-                if more:
-                    gate_step(b + 1, n - 1)
-                blend(b, 1, n, n + 1)
+            blend(b, 1, 0, 2)
             if more:
+                gate_step(b + 1, 0)
+            blend(b, 1, 2, 3)
+            if more:
+                gate_step(b + 1, 1)
+            blend(b, 1, 3, N_TILES)
+            if more:
+                gate_step(b + 1, 2)
                 gate_step(b + 1, 3)
                 gate_step(b + 1, 4)

@@ -29,6 +29,7 @@ EPS = 1e-10
 AHEAD = 2
 PIECES = 8
 LOG2_E = 1.0 / math.log(2.0)
+GATE_STEP = 16
 VALUES_ON_GPSIMD = (0, 1, 2)
 VALUES_ON_SCALAR = ()
 
@@ -65,10 +66,10 @@ def tile_auxiliarygovernedattention_pa_kernel(
         nc.sync.dma_start(out=rel_rows[0:1, :], in_=reliability.rearrange("(o n) -> o n", o=1))
         q_sb = resident.tile([P, B, TT, D], BF16)
         nc.sync.dma_start(out=q_sb[:], in_=query.rearrange("b (p t) d -> p b t d", t=TT))
-        w1_bf = const.tile([P, 1], BF16)
-        bias_bf = const.tile([P, 1], BF16)
-        nc.sync.dma_start(out=w1_bf[:], in_=gate_w1.partition_broadcast(P))
-        nc.sync.dma_start(out=bias_bf[:], in_=gate_bias.partition_broadcast(P))
+        gate_rows = const.tile([P, 2 * GATE_STEP], BF16)
+        nc.vector.memset(gate_rows[:], 0.0)
+        nc.sync.dma_start(out=gate_rows[0:1, 0:1], in_=gate_w1.rearrange("(o n) -> o n", o=1))
+        nc.sync.dma_start(out=gate_rows[0:1, GATE_STEP : GATE_STEP + 1], in_=gate_bias.rearrange("(o n) -> o n", o=1))
         val_raw = resident.tile([P, PACK, H], BF16)
         val_view = aux_values.rearrange("(p j) w -> p j w", j=PACK)
         for half in range(2):
@@ -106,14 +107,6 @@ def tile_auxiliarygovernedattention_pa_kernel(
         )
         head_mean_sel = const.tile([P, S_HI], BF16)
         nc.vector.tensor_scalar_mul(out=head_mean_sel[:], in0=head_count[:], scalar1=1.0 / NH)
-        w1_neg = const.tile([P, 1], F32)
-        nc.gpsimd.tensor_scalar(
-            out=w1_neg[:], in0=w1_bf[:], scalar1=-LOG2_E, scalar2=0.0, op0=ALU.mult, op1=ALU.add
-        )
-        bias_neg = const.tile([P, 1], F32)
-        nc.gpsimd.tensor_scalar(
-            out=bias_neg[:], in0=bias_bf[:], scalar1=-LOG2_E, scalar2=0.0, op0=ALU.mult, op1=ALU.add
-        )
         twos = const.tile([P, TT], F32)
         nc.gpsimd.memset(twos[:], 2.0)
 
@@ -138,6 +131,17 @@ def tile_auxiliarygovernedattention_pa_kernel(
                 nc.tensor.transpose(q_ps[:, b * TT + t, :], q_sb[:, b, t, :], ident[:])
         q_t = resident.tile([P, B * TT, P], BF16)
         nc.vector.tensor_copy(out=q_t[:], in_=q_ps[:])
+        gate_ps = bank([P, 2 * GATE_STEP], F32, "gate_ps")
+        nc.tensor.matmul(gate_ps[:], lhsT=ones[:], rhs=gate_rows[:], start=True, stop=True)
+        gate_coef = const.tile([P, 2], F32)
+        nc.vector.tensor_scalar(
+            out=gate_coef[:],
+            in0=gate_ps[:].rearrange("p (c g) -> p c g", g=GATE_STEP)[:, :, 0],
+            scalar1=-LOG2_E,
+            scalar2=0.0,
+            op0=ALU.mult,
+            op1=ALU.add,
+        )
 
         attn_codes = resident.tile([P, B * TT * P], U32, align_bytes=64)
         attn_scales = resident.tile([P, B * TT * P], U8, align_bytes=64)
@@ -317,7 +321,12 @@ def tile_auxiliarygovernedattention_pa_kernel(
             if step == 0:
                 x = work.tile([P, TT], F32)
                 nc.vector.tensor_scalar(
-                    out=x[:], in0=ent_ps[b][:], scalar1=w1_neg[:], scalar2=bias_neg[:], op0=ALU.mult, op1=ALU.add
+                    out=x[:],
+                    in0=ent_ps[b][:],
+                    scalar1=gate_coef[:, 0:1],
+                    scalar2=gate_coef[:, 1:2],
+                    op0=ALU.mult,
+                    op1=ALU.add,
                 )
                 two_to_x[b] = work.tile([P, TT], F32, name="two_to_x")
                 nc.gpsimd.tensor_tensor(out=two_to_x[b][:], in0=twos[:], in1=x[:], op=ALU.pow)

@@ -71,10 +71,7 @@ def tile_auxiliarygovernedattention_pa_kernel(
         nc.sync.dma_start(out=gate_rows[0:1, 0:1], in_=gate_w1.rearrange("(o n) -> o n", o=1))
         nc.sync.dma_start(out=gate_rows[0:1, GATE_STEP : GATE_STEP + 1], in_=gate_bias.rearrange("(o n) -> o n", o=1))
         val_raw = resident.tile([P, PACK, H], BF16)
-        val_view = aux_values.rearrange("(p j) w -> p j w", j=PACK)
-        for half in range(2):
-            cols = slice(half * H // 2, (half + 1) * H // 2)
-            nc.sync.dma_start(out=val_raw[:, :, cols], in_=val_view[:, :, cols])
+        nc.sync.dma_start(out=val_raw[:], in_=aux_values.rearrange("(p j) w -> p j w", j=PACK))
         paw_view = primary_attention_weights.rearrange("b h (sh sl) k -> b (h sh) sl k", sh=S_HI)
         pao_view = primary_attention_output.rearrange("b (p t) h -> b p t h", t=TT)
         out_view = out.rearrange("b (p t) h -> b p t h", t=TT)
@@ -83,9 +80,7 @@ def tile_auxiliarygovernedattention_pa_kernel(
         for b in range(B + 1):
             if b < B:
                 paw_sb.append(resident.tile([P, S_LO, S], BF16, name="paw%d" % b, tag="stream", bufs=B))
-                for half in range(2):
-                    rows = slice(half * S_LO // 2, (half + 1) * S_LO // 2)
-                    nc.sync.dma_start(out=paw_sb[b][:, rows, :], in_=paw_view[b][:, rows, :])
+                nc.sync.dma_start(out=paw_sb[b][:], in_=paw_view[b])
             if b >= 1:
                 pao_sb.append(resident.tile([P, TT, H], BF16, name="pao%d" % (b - 1)))
                 nc.sync.dma_start(out=pao_sb[b - 1][:], in_=pao_view[b - 1])

@@ -29,6 +29,7 @@ EPS = 1e-10
 AHEAD = 2
 PIECES = 8
 LOG2_E = 1.0 / math.log(2.0)
+EARLY = 2
 GATE_STEP = 16
 VALUES_ON_GPSIMD = (0, 1, 2)
 VALUES_ON_SCALAR = ()
@@ -64,8 +65,10 @@ def tile_auxiliarygovernedattention_pa_kernel(
         keys_sb = resident.tile([P, PACK, D], BF16)
         nc.sync.dma_start(out=keys_sb[:], in_=aux_keys.rearrange("(p c) d -> p c d", c=PACK))
         nc.sync.dma_start(out=rel_rows[0:1, :], in_=reliability.rearrange("(o n) -> o n", o=1))
+        q_view = query.rearrange("b (p t) d -> p b t d", t=TT)
         q_sb = resident.tile([P, B, TT, D], BF16)
-        nc.sync.dma_start(out=q_sb[:], in_=query.rearrange("b (p t) d -> p b t d", t=TT))
+        nc.sync.dma_start(out=q_sb[:, 0:EARLY], in_=q_view[:, 0:EARLY])
+        nc.sync.dma_start(out=q_sb[:, EARLY:B], in_=q_view[:, EARLY:B])
         gate_rows = const.tile([P, 2 * GATE_STEP], BF16)
         nc.vector.memset(gate_rows[:], 0.0)
         nc.sync.dma_start(out=gate_rows[0:1, 0:1], in_=gate_w1.rearrange("(o n) -> o n", o=1))
@@ -105,11 +108,9 @@ def tile_auxiliarygovernedattention_pa_kernel(
         twos = const.tile([P, TT], F32)
         nc.gpsimd.memset(twos[:], 2.0)
 
-        keys_ps = bank([P, PACK, P], BF16, "keys_ps")
+        first_ps = bank([P, PACK + EARLY * TT, P], BF16, "first_ps")
         for c in range(PACK):
-            nc.tensor.transpose(keys_ps[:, c, :], keys_sb[:, c, :], ident[:])
-        keys_t = resident.tile([P, PACK, P], BF16)
-        nc.vector.tensor_copy(out=keys_t[:], in_=keys_ps[:])
+            nc.tensor.transpose(first_ps[:, c, :], keys_sb[:, c, :], ident[:])
         rel_ps = bank([P, NS], F32, "rel_ps")
         nc.tensor.matmul(rel_ps[:], lhsT=ones[:], rhs=rel_rows[:], start=True, stop=True)
         log_rel = resident.tile([P, PACK, P], F32)
@@ -120,23 +121,13 @@ def tile_auxiliarygovernedattention_pa_kernel(
             bias=eps[:],
             scale=1.0,
         )
-        q_ps = bank([P, B * TT, P], BF16, "q_ps")
-        for b in range(B):
+        for b in range(EARLY):
             for t in range(TT):
-                nc.tensor.transpose(q_ps[:, b * TT + t, :], q_sb[:, b, t, :], ident[:])
-        q_t = resident.tile([P, B * TT, P], BF16)
-        nc.vector.tensor_copy(out=q_t[:], in_=q_ps[:])
-        gate_ps = bank([P, 2 * GATE_STEP], F32, "gate_ps")
-        nc.tensor.matmul(gate_ps[:], lhsT=ones[:], rhs=gate_rows[:], start=True, stop=True)
+                nc.tensor.transpose(first_ps[:, PACK + b * TT + t, :], q_sb[:, b, t, :], ident[:])
+        first_t = resident.tile([P, PACK + EARLY * TT, P], BF16)
+        nc.vector.tensor_copy(out=first_t[:], in_=first_ps[:])
+        q_t = resident.tile([P, (B - EARLY) * TT, P], BF16)
         gate_coef = const.tile([P, 2], F32)
-        nc.vector.tensor_scalar(
-            out=gate_coef[:],
-            in0=gate_ps[:].rearrange("p (c g) -> p c g", g=GATE_STEP)[:, :, 0],
-            scalar1=-LOG2_E,
-            scalar2=0.0,
-            op0=ALU.mult,
-            op1=ALU.add,
-        )
 
         attn_codes = resident.tile([P, B * TT * P], U32, align_bytes=64)
         attn_scales = resident.tile([P, B * TT * P], U8, align_bytes=64)
@@ -165,13 +156,32 @@ def tile_auxiliarygovernedattention_pa_kernel(
         aux_ps = {}
         mixed = {}
 
+        def other_queries():
+            q_ps = bank([P, (B - EARLY) * TT, P], BF16, "q_ps")
+            for b in range(EARLY, B):
+                for t in range(TT):
+                    nc.tensor.transpose(q_ps[:, (b - EARLY) * TT + t, :], q_sb[:, b, t, :], ident[:])
+            nc.scalar.copy(out=q_t[:], in_=q_ps[:])
+
+        def gate_coefficients():
+            gate_ps = bank([P, 2 * GATE_STEP], F32, "gate_ps")
+            nc.tensor.matmul(gate_ps[:], lhsT=ones[:], rhs=gate_rows[:], start=True, stop=True)
+            nc.vector.tensor_scalar(
+                out=gate_coef[:],
+                in0=gate_ps[:].rearrange("p (c g) -> p c g", g=GATE_STEP)[:, :, 0],
+                scalar1=-LOG2_E,
+                scalar2=0.0,
+                op0=ALU.mult,
+                op1=ALU.add,
+            )
+
         def scores(b):
             for t in range(TT):
                 score_ps[(b, t)] = bank([P, NS], F32, "score_ps")
                 nc.tensor.matmul(
                     score_ps[(b, t)][:],
-                    lhsT=q_t[:, b * TT + t, :],
-                    rhs=keys_t[:].rearrange("d c j -> d (c j)"),
+                    lhsT=first_t[:, PACK + b * TT + t, :] if b < EARLY else q_t[:, (b - EARLY) * TT + t, :],
+                    rhs=first_t[:, 0:PACK, :].rearrange("d c j -> d (c j)"),
                     start=True,
                     stop=True,
                 )
@@ -390,6 +400,8 @@ def tile_auxiliarygovernedattention_pa_kernel(
         logits(0)
         maxima(0)
         exponentials(0)
+        other_queries()
+        gate_coefficients()
         scores(2)
         logits(1)
         invert_sums(0)

@@ -401,7 +401,6 @@ def tile_auxiliarygovernedattention_pa_kernel(
         maxima(0)
         exponentials(0)
         other_queries()
-        gate_coefficients()
         scores(2)
         logits(1)
         invert_sums(0)
@@ -422,6 +421,7 @@ def tile_auxiliarygovernedattention_pa_kernel(
         invert_sums(2)
         maxima(3)
         exponentials(3)
+        gate_coefficients()
         for piece in range(PIECES):
             head_mean(1, piece)
         log_of_head_mean(0)

@@ -387,11 +387,11 @@ def tile_auxiliarygovernedattention_pa_kernel(
                     op0=ALU.mult,
                     op1=ALU.add,
                 )
-            if (b, t) == (B - 1, TT - 1):
-                cols = slice(n_from * N_TILE, n_to * N_TILE)
-                nc.sync.dma_start(out=out_view[b, :, t, cols], in_=mixed[b][:, t, cols])
-            elif n_to == N_TILES:
-                nc.sync.dma_start(out=out_view[b, :, t, :], in_=mixed[b][:, t, :])
+            group = N_TILES if b < B // 2 else (1 if (b, t) == (B - 1, TT - 1) else 2)
+            for n in range(n_from, n_to):
+                if (n + 1) % group == 0:
+                    cols = slice((n + 1 - group) * N_TILE, (n + 1) * N_TILE)
+                    nc.sync.dma_start(out=out_view[b, :, t, cols], in_=mixed[b][:, t, cols])
 
         for n in VALUES_ON_GPSIMD:
             regroup_values(n)

@@ -111,6 +111,11 @@ def tile_auxiliarygovernedattention_pa_kernel(
         first_ps = bank([P, PACK + EARLY * TT, P], BF16, "first_ps")
         for c in range(PACK):
             nc.tensor.transpose(first_ps[:, c, :], keys_sb[:, c, :], ident[:])
+        for b in range(EARLY):
+            for t in range(TT):
+                nc.tensor.transpose(first_ps[:, PACK + b * TT + t, :], q_sb[:, b, t, :], ident[:])
+        first_t = resident.tile([P, PACK + EARLY * TT, P], BF16)
+        nc.vector.tensor_copy(out=first_t[:], in_=first_ps[:])
         rel_ps = bank([P, NS], F32, "rel_ps")
         nc.tensor.matmul(rel_ps[:], lhsT=ones[:], rhs=rel_rows[:], start=True, stop=True)
         log_rel = resident.tile([P, PACK, P], F32)
@@ -121,11 +126,6 @@ def tile_auxiliarygovernedattention_pa_kernel(
             bias=eps[:],
             scale=1.0,
         )
-        for b in range(EARLY):
-            for t in range(TT):
-                nc.tensor.transpose(first_ps[:, PACK + b * TT + t, :], q_sb[:, b, t, :], ident[:])
-        first_t = resident.tile([P, PACK + EARLY * TT, P], BF16)
-        nc.vector.tensor_copy(out=first_t[:], in_=first_ps[:])
         q_t = resident.tile([P, (B - EARLY) * TT, P], BF16)
         gate_coef = const.tile([P, 2], F32)
 
@@ -134,6 +134,7 @@ def tile_auxiliarygovernedattention_pa_kernel(
         val_codes = resident.tile([P, H], U32, align_bytes=64)
         val_scales = resident.tile([P, H], U8, align_bytes=64)
 
+        gate_ps = {}
         score_ps = {}
         logit = {}
         neg_max = {}
@@ -163,12 +164,14 @@ def tile_auxiliarygovernedattention_pa_kernel(
                     nc.tensor.transpose(q_ps[:, (b - EARLY) * TT + t, :], q_sb[:, b, t, :], ident[:])
             nc.scalar.copy(out=q_t[:], in_=q_ps[:])
 
-        def gate_coefficients():
-            gate_ps = bank([P, 2 * GATE_STEP], F32, "gate_ps")
-            nc.tensor.matmul(gate_ps[:], lhsT=ones[:], rhs=gate_rows[:], start=True, stop=True)
+        def spread_gate_coefficients():
+            gate_ps[0] = bank([P, 2 * GATE_STEP], F32, "gate_ps")
+            nc.tensor.matmul(gate_ps[0][:], lhsT=ones[:], rhs=gate_rows[:], start=True, stop=True)
+
+        def scale_gate_coefficients():
             nc.vector.tensor_scalar(
                 out=gate_coef[:],
-                in0=gate_ps[:].rearrange("p (c g) -> p c g", g=GATE_STEP)[:, :, 0],
+                in0=gate_ps[0][:].rearrange("p (c g) -> p c g", g=GATE_STEP)[:, :, 0],
                 scalar1=-LOG2_E,
                 scalar2=0.0,
                 op0=ALU.mult,
@@ -409,6 +412,7 @@ def tile_auxiliarygovernedattention_pa_kernel(
         exponentials(1)
         normalise(0, 1)
         scores(3)
+        spread_gate_coefficients()
         logits(2)
         invert_sums(1)
         maxima(2)
@@ -421,7 +425,6 @@ def tile_auxiliarygovernedattention_pa_kernel(
         invert_sums(2)
         maxima(3)
         exponentials(3)
-        gate_coefficients()
         for piece in range(PIECES):
             head_mean(1, piece)
         log_of_head_mean(0)
@@ -436,6 +439,7 @@ def tile_auxiliarygovernedattention_pa_kernel(
         entropy(0)
         quantise_values(2)
         quantise_attention(0)
+        scale_gate_coefficients()
         gate_step(0, 0)
         quantise_values(3)
         products(0, 0)

import math
from contextlib import ExitStack

import concourse.mybir as mybir
from concourse.masks import make_identity

F32 = mybir.dt.float32
BF16 = mybir.dt.bfloat16
U32 = mybir.dt.uint32
U8 = mybir.dt.uint8
FP8X4 = mybir.dt.float8_e4m3fn_x4
ALU = mybir.AluOpType
FUNC = mybir.ActivationFunctionType
AXIS_X = mybir.AxisListType.X

P = 128
PACK = 4
B, S, H, NH, NS, D = 4, 256, 2048, 16, 512, 128
TT = S // P
N_TILE = 512
N_TILES = H // N_TILE
KH = S // P
S_HI = P // NH
S_LO = S // S_HI
TAU_LOW = 0.5
TAU_HIGH = 2.0
GATE_CAP = 0.8
EPS = 1e-10
AHEAD = 2
PIECES = 8
LOG2_E = 1.0 / math.log(2.0)
EARLY = 2
GATE_STEP = 16
VALUES_ON_GPSIMD = (0, 1, 2)
VALUES_ON_SCALAR = ()

FLOPS = 2 * B * S * NS * (D + H)


def tile_auxiliarygovernedattention_pa_kernel(
    tc,
    query,
    aux_keys,
    aux_values,
    reliability,
    primary_attention_weights,
    primary_attention_output,
    gate_w1,
    gate_bias,
    out,
):
    nc = tc.nc
    with ExitStack() as ctx:
        ctx.enter_context(tc.manual_schedule())
        const = ctx.enter_context(tc.tile_pool(name="const", bufs=1))
        resident = ctx.enter_context(tc.tile_pool(name="resident", bufs=1))
        work = ctx.enter_context(tc.tile_pool(name="work", bufs=2))
        psum = ctx.enter_context(tc.psum_pool(name="psum", bufs=1))

        def bank(shape, dtype, name):
            return psum.tile(shape, dtype, name=name, tag="bank", bufs=4)

        rel_rows = const.tile([P, NS], BF16)
        nc.vector.memset(rel_rows[:], 0.0)
        keys_sb = resident.tile([P, PACK, D], BF16)
        nc.sync.dma_start(out=keys_sb[:], in_=aux_keys.rearrange("(p c) d -> p c d", c=PACK))
        nc.sync.dma_start(out=rel_rows[0:1, :], in_=reliability.rearrange("(o n) -> o n", o=1))
        q_view = query.rearrange("b (p t) d -> p b t d", t=TT)
        q_sb = resident.tile([P, B, TT, D], BF16)
        nc.sync.dma_start(out=q_sb[:, 0:EARLY], in_=q_view[:, 0:EARLY])
        nc.sync.dma_start(out=q_sb[:, EARLY:B], in_=q_view[:, EARLY:B])
        gate_rows = const.tile([P, 2 * GATE_STEP], BF16)
        nc.vector.memset(gate_rows[:], 0.0)
        nc.sync.dma_start(out=gate_rows[0:1, 0:1], in_=gate_w1.rearrange("(o n) -> o n", o=1))
        nc.sync.dma_start(out=gate_rows[0:1, GATE_STEP : GATE_STEP + 1], in_=gate_bias.rearrange("(o n) -> o n", o=1))
        val_raw = resident.tile([P, PACK, H], BF16)
        nc.sync.dma_start(out=val_raw[:], in_=aux_values.rearrange("(p j) w -> p j w", j=PACK))
        paw_view = primary_attention_weights.rearrange("b h (sh sl) k -> b (h sh) sl k", sh=S_HI)
        pao_view = primary_attention_output.rearrange("b (p t) h -> b p t h", t=TT)
        out_view = out.rearrange("b (p t) h -> b p t h", t=TT)
        paw_sb = []
        pao_sb = []
        for b in range(B + 1):
            if b < B:
                paw_sb.append(resident.tile([P, S_LO, S], BF16, name="paw%d" % b, tag="stream", bufs=B))
                nc.sync.dma_start(out=paw_sb[b][:], in_=paw_view[b])
            if b >= 1:
                pao_sb.append(resident.tile([P, TT, H], BF16, name="pao%d" % (b - 1)))
                nc.sync.dma_start(out=pao_sb[b - 1][:], in_=pao_view[b - 1])

        ident = const.tile([P, P], BF16)
        make_identity(nc, ident[:])
        ones = const.tile([P, P], BF16)
        nc.vector.memset(ones[:], 1.0)
        eps = const.tile([P, 1], F32)
        nc.vector.memset(eps[:], EPS)
        minus_ones = const.tile([P, 1], F32)
        nc.vector.memset(minus_ones[:], -1.0)
        head_count = const.tile([P, S_HI], F32)
        nc.vector.tensor_reduce(
            out=head_count[:],
            in_=ident[:].rearrange("p (h n) -> p n h", n=S_HI),
            axis=AXIS_X,
            op=ALU.add,
        )
        head_mean_sel = const.tile([P, S_HI], BF16)
        nc.vector.tensor_scalar_mul(out=head_mean_sel[:], in0=head_count[:], scalar1=1.0 / NH)
        twos = const.tile([P, TT], F32)
        nc.gpsimd.memset(twos[:], 2.0)

        first_ps = bank([P, PACK + EARLY * TT, P], BF16, "first_ps")
        for c in range(PACK):
            nc.tensor.transpose(first_ps[:, c, :], keys_sb[:, c, :], ident[:])
        for b in range(EARLY):
            for t in range(TT):
                nc.tensor.transpose(first_ps[:, PACK + b * TT + t, :], q_sb[:, b, t, :], ident[:])
        first_t = resident.tile([P, PACK + EARLY * TT, P], BF16)
        nc.vector.tensor_copy(out=first_t[:], in_=first_ps[:])
        rel_ps = bank([P, NS], F32, "rel_ps")
        nc.tensor.matmul(rel_ps[:], lhsT=ones[:], rhs=rel_rows[:], start=True, stop=True)
        log_rel = resident.tile([P, PACK, P], F32)
        nc.scalar.activation(
            out=log_rel[:],
            in_=rel_ps[:].rearrange("p (j c) -> p c j", c=PACK),
            func=FUNC.Ln,
            bias=eps[:],
            scale=1.0,
        )
        q_t = resident.tile([P, (B - EARLY) * TT, P], BF16)
        gate_coef = const.tile([P, 2], F32)

        attn_codes = resident.tile([P, B * TT * P], U32, align_bytes=64)
        attn_scales = resident.tile([P, B * TT * P], U8, align_bytes=64)
        val_codes = resident.tile([P, H], U32, align_bytes=64)
        val_scales = resident.tile([P, H], U8, align_bytes=64)

        gate_ps = {}
        score_ps = {}
        logit = {}
        neg_max = {}
        exp_sum = {}
        inv_sum = {}
        attn = {}
        attn_ps = {}
        attn_grouped = {}
        val_grouped = {}
        avg_ps = {}
        log_avg = {}
        terms = {}
        ent_ps = {}
        cap = {}
        limit = {}
        denom = {}
        sigmoid = {}
        two_to_x = {}
        gate = {}
        aux_ps = {}
        mixed = {}

        def other_queries():
            q_ps = bank([P, (B - EARLY) * TT, P], BF16, "q_ps")
            for b in range(EARLY, B):
                for t in range(TT):
                    nc.tensor.transpose(q_ps[:, (b - EARLY) * TT + t, :], q_sb[:, b, t, :], ident[:])
            nc.scalar.copy(out=q_t[:], in_=q_ps[:])

        def spread_gate_coefficients():
            gate_ps[0] = bank([P, 2 * GATE_STEP], F32, "gate_ps")
            nc.tensor.matmul(gate_ps[0][:], lhsT=ones[:], rhs=gate_rows[:], start=True, stop=True)

        def scale_gate_coefficients():
            nc.vector.tensor_scalar(
                out=gate_coef[:],
                in0=gate_ps[0][:].rearrange("p (c g) -> p c g", g=GATE_STEP)[:, :, 0],
                scalar1=-LOG2_E,
                scalar2=0.0,
                op0=ALU.mult,
                op1=ALU.add,
            )

        def scores(b):
            for t in range(TT):
                score_ps[(b, t)] = bank([P, NS], F32, "score_ps")
                nc.tensor.matmul(
                    score_ps[(b, t)][:],
                    lhsT=first_t[:, PACK + b * TT + t, :] if b < EARLY else q_t[:, (b - EARLY) * TT + t, :],
                    rhs=first_t[:, 0:PACK, :].rearrange("d c j -> d (c j)"),
                    start=True,
                    stop=True,
                )

        def logits(b):
            logit[b] = work.tile([P, TT, NS], F32, name="logit", bufs=B)
            for t in range(TT):
                nc.vector.scalar_tensor_tensor(
                    out=logit[b][:, t, :],
                    in0=score_ps[(b, t)][:],
                    scalar=1.0 / math.sqrt(D),
                    in1=log_rel[:].rearrange("p c j -> p (c j)"),
                    op0=ALU.mult,
                    op1=ALU.add,
                )

        def maxima(b):
            neg_max[b] = work.tile([P, TT], F32, name="neg_max", bufs=B)
            for t in range(TT):
                nc.vector.tensor_reduce(
                    out=neg_max[b][:, t : t + 1], in_=logit[b][:, t, :], axis=AXIS_X, op=ALU.max, negate=True
                )

        def exponentials(b):
            exp_sum[b] = work.tile([P, TT], F32, name="exp_sum", bufs=B)
            for t in range(TT):
                nc.scalar.activation(
                    out=logit[b][:, t, :],
                    in_=logit[b][:, t, :],
                    func=FUNC.Exp,
                    bias=neg_max[b][:, t : t + 1],
                    scale=1.0,
                    accum_out=exp_sum[b][:, t : t + 1],
                )

        def invert_sums(b):
            inv_sum[b] = work.tile([P, TT], F32, name="inv_sum", bufs=B)
            nc.vector.reciprocal(out=inv_sum[b][:], in_=exp_sum[b][:])

        def normalise(b, t):
            if t == 0:
                attn[b] = work.tile([P, TT, PACK, P], BF16, name="attn", bufs=B)
            nc.scalar.activation(
                out=attn[b][:, t].rearrange("p c j -> p (c j)"),
                in_=logit[b][:, t, :],
                func=FUNC.Copy,
                scale=inv_sum[b][:, t : t + 1],
            )

        def transpose_attention(b):
            attn_ps[b] = psum.tile([P, TT, PACK, P], BF16, name="attn_ps")
            for t in range(TT):
                for c in range(PACK):
                    nc.tensor.transpose(attn_ps[b][:, t, c, :], attn[b][:, t, c, :], ident[:])

        def regroup_attention(b):
            attn_grouped[b] = work.tile([P, TT, P, PACK], BF16, name="attn_grouped", bufs=B, align_bytes=64)
            nc.scalar.copy(out=attn_grouped[b][:], in_=attn_ps[b][:].rearrange("p t c k -> p t k c"))

        def quantise_attention(b):
            cols = slice(b * TT * P, (b + 1) * TT * P)
            nc.vector.quantize_mx(
                out=attn_codes[:, cols].bitcast(FP8X4),
                scales=attn_scales[:, cols],
                in_=attn_grouped[b][:].rearrange("p t k c -> p (t k c)"),
            )

        def regroup_values(n):
            cols = slice(n * N_TILE, (n + 1) * N_TILE)
            val_grouped[n] = work.tile([P, N_TILE, PACK], BF16, name="val_grouped", bufs=N_TILES, align_bytes=64)
            if n in VALUES_ON_GPSIMD:
                nc.gpsimd.tensor_scalar(
                    out=val_grouped[n][:],
                    in0=val_raw[:, :, cols].rearrange("p j w -> p w j"),
                    scalar1=1.0,
                    scalar2=0.0,
                    op0=ALU.mult,
                    op1=ALU.add,
                )
            elif n in VALUES_ON_SCALAR:
                nc.scalar.copy(out=val_grouped[n][:], in_=val_raw[:, :, cols].rearrange("p j w -> p w j"))
            else:
                nc.vector.tensor_copy(
                    out=val_grouped[n][:].rearrange("p (w i) j -> p w j i", i=4),
                    in_=val_raw[:, :, cols].rearrange("p j (w i) -> p w j i", i=4),
                )

        def quantise_values(n):
            cols = slice(n * N_TILE, (n + 1) * N_TILE)
            nc.vector.quantize_mx(
                out=val_codes[:, cols].bitcast(FP8X4),
                scales=val_scales[:, cols],
                in_=val_grouped[n][:].rearrange("p w j -> p (w j)"),
            )

        def head_mean(b, piece):
            if piece == 0:
                avg_ps[b] = psum.tile([P, KH, TT, P], F32, name="avg_ps", bufs=2)
            avg_cols = avg_ps[b][:].rearrange("k kh t (sh j) -> k kh t j sh", sh=S_HI)
            for s_lo in range(piece * S_LO // PIECES, (piece + 1) * S_LO // PIECES):
                for kh in range(KH):
                    nc.tensor.matmul(
                        avg_cols[:, kh, s_lo % TT, s_lo // TT, :],
                        lhsT=paw_sb[b][:, s_lo, kh * P : (kh + 1) * P],
                        rhs=head_mean_sel[:],
                        start=True,
                        stop=True,
                    )

        def log_of_head_mean(b):
            log_avg[b] = work.tile([P, KH * TT * P], F32, name="log_avg", bufs=AHEAD)
            nc.scalar.activation(
                out=log_avg[b][:],
                in_=avg_ps[b][:].rearrange("k kh t p -> k (kh t p)"),
                func=FUNC.Ln,
                bias=eps[:],
                scale=1.0,
            )

        def entropy_terms(b):
            terms[b] = work.tile([P, KH, TT, P], F32, name="terms")
            nc.vector.tensor_tensor(
                out=terms[b][:].rearrange("k kh t p -> k (kh t p)"),
                in0=avg_ps[b][:].rearrange("k kh t p -> k (kh t p)"),
                in1=log_avg[b][:],
                op=ALU.mult,
            )

        def entropy(b):
            ent_ps[b] = psum.tile([P, TT], F32, name="ent_ps")
            for t in range(TT):
                for kh in range(KH):
                    nc.tensor.matmul(
                        ent_ps[b][:, t : t + 1],
                        lhsT=terms[b][:, kh, t, :],
                        rhs=minus_ones[:],
                        start=(kh == 0),
                        stop=(kh == KH - 1),
                    )

        def gate_step(b, step):
            if step == 0:
                x = work.tile([P, TT], F32)
                nc.vector.tensor_scalar(
                    out=x[:],
                    in0=ent_ps[b][:],
                    scalar1=gate_coef[:, 0:1],
                    scalar2=gate_coef[:, 1:2],
                    op0=ALU.mult,
                    op1=ALU.add,
                )
                two_to_x[b] = work.tile([P, TT], F32, name="two_to_x")
                nc.gpsimd.tensor_tensor(out=two_to_x[b][:], in0=twos[:], in1=x[:], op=ALU.pow)
                cap[b] = work.tile([P, TT], F32, name="cap")
                nc.vector.tensor_scalar(
                    out=cap[b][:], in0=ent_ps[b][:], scalar1=TAU_HIGH, scalar2=GATE_CAP, op0=ALU.is_le, op1=ALU.max
                )
            elif step == 1:
                limit[b] = work.tile([P, TT], F32, name="limit")
                nc.vector.scalar_tensor_tensor(
                    out=limit[b][:], in0=ent_ps[b][:], scalar=TAU_LOW, in1=cap[b][:], op0=ALU.is_ge, op1=ALU.mult
                )
            elif step == 2:
                denom[b] = work.tile([P, TT], F32, name="denom")
                nc.vector.tensor_scalar_add(out=denom[b][:], in0=two_to_x[b][:], scalar1=1.0)
            elif step == 3:
                sigmoid[b] = work.tile([P, TT], F32, name="sigmoid")
                nc.vector.reciprocal(out=sigmoid[b][:], in_=denom[b][:])
            else:
                gate[b] = work.tile([P, TT], F32, name="gate")
                nc.vector.tensor_tensor(out=gate[b][:], in0=sigmoid[b][:], in1=limit[b][:], op=ALU.min)

        def products(b, t, averaged=B, first_piece=0, per_pass=1, entropy_after=N_TILES):
            toks = slice((b * TT + t) * P, (b * TT + t + 1) * P)
            for n in range(N_TILES):
                cols = slice(n * N_TILE, (n + 1) * N_TILE)
                aux_ps[(b, t, n)] = bank([P, N_TILE], F32, "aux_ps")
                nc.tensor.matmul_mx(
                    out=aux_ps[(b, t, n)][:],
                    lhsT=attn_codes[:, toks].bitcast(FP8X4),
                    lhsT_scale=attn_scales[:, toks],
                    rhs=val_codes[:, cols].bitcast(FP8X4),
                    rhs_scale=val_scales[:, cols],
                    start=True,
                    stop=True,
                )
                if averaged < B:
                    for piece in range(first_piece + n * per_pass, first_piece + (n + 1) * per_pass):
                        head_mean(averaged, piece)
                if n == entropy_after and b + 1 < B:
                    entropy(b + 1)

        def blend(b, t, n_from, n_to):
            if t == 0 and n_from == 0:
                mixed[b] = resident.tile([P, TT, H], F32, name="mixed%d" % b, tag="stream", bufs=B)
            for n in range(n_from, n_to):
                cols = slice(n * N_TILE, (n + 1) * N_TILE)
                nc.vector.scalar_tensor_tensor(
                    out=mixed[b][:, t, cols],
                    in0=aux_ps[(b, t, n)][:],
                    scalar=gate[b][:, t : t + 1],
                    in1=pao_sb[b][:, t, cols],
                    op0=ALU.mult,
                    op1=ALU.add,
                )
            group = N_TILES if b < B // 2 else (1 if (b, t) == (B - 1, TT - 1) else 2)
            for n in range(n_from, n_to):
                if (n + 1) % group == 0:
                    cols = slice((n + 1 - group) * N_TILE, (n + 1) * N_TILE)
                    nc.sync.dma_start(out=out_view[b, :, t, cols], in_=mixed[b][:, t, cols])

        for n in VALUES_ON_GPSIMD:
            regroup_values(n)
        scores(0)
        scores(1)
        logits(0)
        maxima(0)
        exponentials(0)
        other_queries()
        scores(2)
        logits(1)
        invert_sums(0)
        normalise(0, 0)
        maxima(1)
        exponentials(1)
        normalise(0, 1)
        scores(3)
        spread_gate_coefficients()
        logits(2)
        invert_sums(1)
        maxima(2)
        exponentials(2)
        normalise(1, 0)
        for piece in range(PIECES):
            head_mean(0, piece)
        transpose_attention(0)
        logits(3)
        invert_sums(2)
        maxima(3)
        exponentials(3)
        for piece in range(PIECES):
            head_mean(1, piece)
        log_of_head_mean(0)
        regroup_attention(0)
        log_of_head_mean(1)
        normalise(1, 1)
        regroup_values(3)
        invert_sums(3)
        quantise_values(0)
        quantise_values(1)
        entropy_terms(0)
        entropy(0)
        quantise_values(2)
        quantise_attention(0)
        scale_gate_coefficients()
        gate_step(0, 0)
        quantise_values(3)
        products(0, 0)
        transpose_attention(1)
        regroup_attention(1)
        normalise(2, 0)
        normalise(2, 1)
        gate_step(0, 1)
        gate_step(0, 2)
        gate_step(0, 3)
        gate_step(0, 4)

        for b in range(B):
            more = b + 1 < B
            products(b, 1, b + 2, 0)
            blend(b, 0, 0, N_TILES)
            if more:
                quantise_attention(b + 1)
                entropy_terms(b + 1)
                entropy(b + 1)
            if b + 2 < B:
                transpose_attention(b + 2)
                regroup_attention(b + 2)
            if b == 0:
                normalise(3, 0)
                normalise(3, 1)
            if more:
                products(b + 1, 0, b + 2, N_TILES)
            if b + 2 < B:
                log_of_head_mean(b + 2)
            blend(b, 1, 0, 2)
            if more:
                gate_step(b + 1, 0)
            blend(b, 1, 2, 3)
            if more:
                gate_step(b + 1, 1)
            blend(b, 1, 3, N_TILES)
            if more:
                gate_step(b + 1, 2)
                gate_step(b + 1, 3)
                gate_step(b + 1, 4)
